import numpy as np
import ml_dtypes


def mxq(x, axis, fmt="e4m3"):
    dtype, down = {"e4m3": (ml_dtypes.float8_e4m3fn, 7), "e5m2": (ml_dtypes.float8_e5m2, 14)}[fmt]
    v = np.moveaxis(np.asarray(x, np.float32).astype(ml_dtypes.bfloat16).astype(np.float64), axis, -1)
    blocks = v.reshape(v.shape[:-1] + (-1, 32))
    amax = np.abs(blocks).max(-1, keepdims=True)
    byte = np.maximum(np.where(amax > 0, np.frexp(amax)[1] - 1 + 127, 0) - down, 1)
    scale = np.exp2(byte - 127.0)
    codes = (blocks / scale).astype(np.float32).astype(dtype).astype(np.float64)
    return np.moveaxis((codes * scale).reshape(v.shape), -1, axis)


WIDE = False


def mx_kscale(k):
    if not WIDE:
        return np.ones(k)
    levels = np.array([10, -10, 5, -5, 0])
    a = np.random.permutation(np.resize(levels, k // 512 * 4)).reshape(k // 512, 4)
    idx = np.arange(k)
    return np.exp2(a[idx // 512, idx % 128 // 32])


BF16 = ml_dtypes.bfloat16


def bf(x):
    return np.asarray(x, np.float32).astype(BF16)


def f64(x):
    return np.asarray(x).astype(np.float64)


B, N, IN_DIM, UNITS, K = 2, 1024, 128, 128, 3
F = IN_DIM + UNITS
NUM_MX = K + 1
ROWS = F * NUM_MX


def setup_inputs():
    tf = mx_kscale(ROWS)[::NUM_MX]
    tr = np.repeat(tf, NUM_MX)[:, None]
    return {"adj": bf(np.random.standard_normal((N, N)) * 0.5 / np.sqrt(N)),
            "x0": bf(np.random.standard_normal((B, N, F)) * 0.8 * tf),
            "x1": bf(np.random.standard_normal((B, N, F)) * 0.4 * tf),
            "x2": bf(np.random.standard_normal((B, N, F)) * 0.9 * tf),
            "u": bf(1.0 / (1.0 + np.exp(-np.random.standard_normal((B, N * UNITS))))),
            "h_prev": bf(np.random.standard_normal((B, N * UNITS))),
            "c_kernel": bf(np.random.standard_normal((ROWS, UNITS)) / np.sqrt(ROWS) / tr),
            "c_bias": bf(np.random.standard_normal(UNITS) * 0.3)}


def reference(adj, x0, x1, x2, u, h_prev, c_kernel, c_bias):
    x0, x1, x2 = f64(x0), f64(x1), f64(x2)
    x3 = 2.0 * (mxq(f64(adj), 1, "e4m3") @ mxq(x2, 1, "e4m3")) - x1
    xk = np.stack([x0, x1, x2, x3], axis=-1).reshape(B * N, ROWS)
    c = np.tanh((mxq(xk, 1, "e4m3") @ mxq(f64(c_kernel), 0, "e4m3")) + f64(c_bias))
    c = c.reshape(B, N * UNITS)
    u = f64(u)
    return u * f64(h_prev) + (1.0 - u) * c

@@ -1,0 +1,249 @@
+from contextlib import ExitStack
+
+import concourse.mybir as mybir
+from concourse.masks import make_identity
+
+F32 = mybir.dt.float32
+BF16 = mybir.dt.bfloat16
+U32 = mybir.dt.uint32
+U8 = mybir.dt.uint8
+FP8X4 = mybir.dt.float8_e4m3fn_x4
+ALU = mybir.AluOpType
+ACT = mybir.ActivationFunctionType
+
+P = 128
+BATCH = 2
+NODES = 1024
+FEATS = 256
+UNITS = 128
+TERMS = 4
+HALVES = FEATS // P
+PASSES = NODES // (4 * P)
+PAIRS = NODES // (2 * P)
+FLOPS = 2 * NODES * NODES * BATCH * FEATS + 2 * BATCH * NODES * TERMS * FEATS * UNITS
+
+
+def tile_gts_gcgrucell_pc_kernel(tc, adj, x0, x1, x2, u, h_prev, c_kernel, c_bias, out):
+    nc = tc.nc
+    adj_v = adj.rearrange("(c p e) m -> c p (e m)", c=PAIRS, p=P, e=2)
+    x0_v = x0.rearrange("b (c p e) f -> c p b (e f)", c=PAIRS, p=P, e=2)
+    x1_v = x1.rearrange("b (c p e) f -> c p b (e f)", c=PAIRS, p=P, e=2)
+    x2_v = x2.rearrange("b (c p e) f -> c p b (e f)", c=PAIRS, p=P, e=2)
+    u_v = u.rearrange("b (c p e j) -> c p b (e j)", c=PAIRS, p=P, e=2, j=UNITS)
+    h_v = h_prev.rearrange("b (c p e j) -> c p b (e j)", c=PAIRS, p=P, e=2, j=UNITS)
+    out_v = out.rearrange("b (c p e j) -> c p b (e j)", c=PAIRS, p=P, e=2, j=UNITS)
+
+    with ExitStack() as ctx:
+        keep = ctx.enter_context(tc.tile_pool(name="keep", bufs=1))
+        work = ctx.enter_context(tc.tile_pool(name="work", bufs=2))
+        psum_tr = ctx.enter_context(tc.psum_pool(name="psum_tr", bufs=5))
+        psum_mx = ctx.enter_context(tc.psum_pool(name="psum_mx", bufs=3))
+
+        adj_sb = [keep.tile([P, 2, NODES], BF16, name="adj%d" % c) for c in range(PAIRS)]
+        x0_sb = [keep.tile([P, BATCH, 2, FEATS], BF16, name="x0_%d" % c) for c in range(PAIRS)]
+        x1_sb = [keep.tile([P, BATCH, 2, FEATS], BF16, name="x1_%d" % c) for c in range(PAIRS)]
+        x2_sb = [keep.tile([P, BATCH, 4, FEATS], BF16, name="x2_%d" % g) for g in range(PASSES)]
+        u_sb = [keep.tile([P, BATCH, 2 * UNITS], BF16, name="u%d" % c) for c in range(PAIRS)]
+        h_sb = [keep.tile([P, BATCH, 2 * UNITS], BF16, name="h%d" % c) for c in range(PAIRS)]
+        ck_sb = keep.tile([P, HALVES, TERMS, UNITS], BF16)
+        bias_rows = keep.tile([P, P], BF16)
+
+        nc.vector.memset(bias_rows[:], 0.0)
+        nc.scalar.dma_start(out=ck_sb[:], in_=c_kernel.rearrange("(h p t) j -> p h (t j)", h=HALVES, p=P, t=TERMS))
+        nc.scalar.dma_start(out=bias_rows[0:1, :], in_=c_bias.rearrange("(o j) -> o j", o=1))
+
+        nc.sync.dma_start(out=adj_sb[0][:], in_=adj_v[0])
+        for c in range(PAIRS):
+            nc.sync.dma_start(out=x2_sb[c // 2][:, :, 2 * (c % 2) : 2 * (c % 2) + 2, :], in_=x2_v[c])
+        for c in range(PAIRS):
+            if c > 0:
+                nc.sync.dma_start(out=adj_sb[c][:], in_=adj_v[c])
+            nc.sync.dma_start(out=x1_sb[c][:], in_=x1_v[c])
+            nc.sync.dma_start(out=x0_sb[c][:], in_=x0_v[c])
+            nc.sync.dma_start(out=u_sb[c][:], in_=u_v[c])
+            nc.sync.dma_start(out=h_sb[c][:], in_=h_v[c])
+
+        ident_bf = keep.tile([P, P], BF16)
+        make_identity(nc, ident_bf[:])
+        ident_f32 = keep.tile([P, P], F32)
+        make_identity(nc, ident_f32[:])
+        warm = keep.tile([P, 1], F32)
+        nc.vector.memset(warm[:], 0.0)
+        nc.scalar.activation(out=warm[:], in_=warm[:], func=ACT.Tanh)
+
+        x2_codes = []
+        x2_scales = []
+        for g in range(PASSES):
+            x2_grouped = keep.tile([P, BATCH, FEATS, 4], BF16, name="x2_grouped%d" % g, align_bytes=64)
+            nc.vector.tensor_copy(out=x2_grouped[:, 0], in_=x2_sb[g][:, 0].rearrange("p t f -> p f t"))
+            nc.scalar.copy(out=x2_grouped[:, 1], in_=x2_sb[g][:, 1].rearrange("p t f -> p f t"))
+            codes = keep.tile([P, BATCH * FEATS], U32, name="x2_codes%d" % g, align_bytes=64)
+            scales = keep.tile([P, BATCH * FEATS], U8, name="x2_scales%d" % g, align_bytes=64)
+            nc.vector.quantize_mx(
+                out=codes[:].bitcast(FP8X4),
+                scales=scales[:],
+                in_=x2_grouped[:].rearrange("p b f t -> p (b f t)"),
+            )
+            x2_codes.append(codes)
+            x2_scales.append(scales)
+
+        adj_codes = {}
+        adj_scales = {}
+        x3_sb = {}
+        xk_codes = {}
+        xk_scales = {}
+        cand_t = {}
+
+        def transpose_adj(c):
+            grouped = work.tile([P, 2, PASSES, P, 2], F32, name="adj_grouped", align_bytes=64)
+            for e in range(2):
+                words = adj_sb[c][:, e, :].bitcast(F32)
+                adj_t = psum_tr.tile([P, PASSES, 2, P], F32, name="adj_t", tag="tr")
+                for g in range(PASSES):
+                    for w in range(2):
+                        first = (2 * g + w) * P
+                        nc.tensor.transpose(adj_t[:, g, w, :], words[:, first : first + P], ident_f32[:])
+                nc.scalar.copy(out=grouped[:, e], in_=adj_t[:].rearrange("p g w n -> p g n w"))
+            codes = work.tile([P, 2, PASSES, P], U32, name="adj_codes", align_bytes=64)
+            scales = work.tile([P, 2, PASSES, P], U8, name="adj_scales", align_bytes=64)
+            nc.vector.quantize_mx(
+                out=codes[:].rearrange("p e g n -> p (e g n)").bitcast(FP8X4),
+                scales=scales[:].rearrange("p e g n -> p (e g n)"),
+                in_=grouped[:].rearrange("p e g n w -> p (e g n w)").bitcast(BF16),
+            )
+            adj_codes[c] = codes
+            adj_scales[c] = scales
+
+        def diffuse(c):
+            x3 = work.tile([P, 2, BATCH, FEATS], BF16, name="x3")
+            for e in range(2):
+                acc = psum_mx.tile([P, BATCH, FEATS], F32, name="acc1", tag="mx")
+                for g in range(PASSES):
+                    nc.tensor.matmul_mx(
+                        out=acc[:].rearrange("p b f -> p (b f)"),
+                        lhsT=adj_codes[c][:, e, g, :].bitcast(FP8X4),
+                        lhsT_scale=adj_scales[c][:, e, g, :],
+                        rhs=x2_codes[g][:].bitcast(FP8X4),
+                        rhs_scale=x2_scales[g][:],
+                        start=(g == 0),
+                        stop=(g == PASSES - 1),
+                    )
+                nc.vector.scalar_tensor_tensor(
+                    out=x3[:, e],
+                    in0=acc[:],
+                    scalar=2.0,
+                    in1=x1_sb[c][:, :, e, :],
+                    op0=ALU.mult,
+                    op1=ALU.subtract,
+                )
+            x3_sb[c] = x3
+
+        def transpose_terms(c):
+            grouped = work.tile([P, BATCH, HALVES, 2 * P, TERMS], BF16, name="xk_grouped", align_bytes=64)
+            codes = work.tile([P, BATCH, HALVES, 2 * P], U32, name="xk_codes", align_bytes=64)
+            scales = work.tile([P, BATCH, HALVES, 2 * P], U8, name="xk_scales", align_bytes=64)
+            for b in range(BATCH):
+                for e in range(2):
+                    terms = [
+                        x0_sb[c][:, b, e, :],
+                        x1_sb[c][:, b, e, :],
+                        x2_sb[c // 2][:, b, 2 * (c % 2) + e, :],
+                        x3_sb[c][:, e, b, :],
+                    ]
+                    xk_t = psum_tr.tile([P, HALVES, TERMS, P], BF16, name="xk_t", tag="tr")
+                    for h in range(HALVES):
+                        for k in range(TERMS):
+                            nc.tensor.transpose(xk_t[:, h, k, :], terms[k][:, h * P : (h + 1) * P], ident_bf[:])
+                    dst = grouped[:, b, :, e * P : (e + 1) * P, :]
+                    src = xk_t[:].rearrange("p h k n -> p h n k")
+                    if (b, e) == (1, 0):
+                        nc.vector.tensor_copy(out=dst, in_=src)
+                    else:
+                        nc.scalar.copy(out=dst, in_=src)
+                if b == 1:
+                    for bb in range(BATCH):
+                        nc.vector.quantize_mx(
+                            out=codes[:, bb].rearrange("p h n -> p (h n)").bitcast(FP8X4),
+                            scales=scales[:, bb].rearrange("p h n -> p (h n)"),
+                            in_=grouped[:, bb].rearrange("p h n k -> p (h n k)"),
+                        )
+            xk_codes[c] = codes
+            xk_scales[c] = scales
+
+        def candidate(c):
+            acc = psum_mx.tile([P, BATCH, 2 * P], F32, name="acc2", tag="mx")
+            for b in range(BATCH):
+                for h in range(HALVES):
+                    nc.tensor.matmul_mx(
+                        out=acc[:, b, :],
+                        lhsT=ck_codes[:, h, :].bitcast(FP8X4),
+                        lhsT_scale=ck_scales[:, h, :],
+                        rhs=xk_codes[c][:, b, h, :].bitcast(FP8X4),
+                        rhs_scale=xk_scales[c][:, b, h, :],
+                        start=(h == 0),
+                        stop=(h == HALVES - 1),
+                    )
+            cand = work.tile([P, BATCH, 2, P], F32, name="cand")
+            nc.scalar.activation(
+                out=cand[:].rearrange("p b e n -> p (b e n)"),
+                in_=acc[:].rearrange("p b n -> p (b n)"),
+                func=ACT.Tanh,
+                bias=bias_col[:],
+                scale=1.0,
+            )
+            cand_t[c] = cand
+
+        def blend(c):
+            cand_n = psum_tr.tile([P, BATCH, 2, UNITS], F32, name="cand_n", tag="tr")
+            for b in range(BATCH):
+                for e in range(2):
+                    nc.tensor.transpose(cand_n[:, b, e, :], cand_t[c][:, b, e, :], ident_f32[:])
+            new_part = work.tile([P, BATCH, 2 * UNITS], F32, name="new_part")
+            nc.vector.tensor_tensor(
+                out=new_part[:].rearrange("p b x -> p (b x)"),
+                in0=cand_n[:].rearrange("p b e j -> p (b e j)"),
+                in1=one_minus_u[c][:].rearrange("p b x -> p (b x)"),
+                op=ALU.mult,
+            )
+            result = work.tile([P, BATCH, 2 * UNITS], F32, name="result")
+            nc.gpsimd.tensor_tensor(out=result[:], in0=new_part[:], in1=old_part[c][:], op=ALU.add)
+            nc.sync.dma_start(out=out_v[c], in_=result[:])
+
+        transpose_adj(0)
+        diffuse(0)
+
+        ck_grouped = keep.tile([P, HALVES, UNITS, TERMS], BF16, align_bytes=64)
+        nc.vector.tensor_copy(out=ck_grouped[:], in_=ck_sb[:].rearrange("p h t j -> p h j t"))
+        ck_codes = keep.tile([P, HALVES, UNITS], U32, align_bytes=64)
+        ck_scales = keep.tile([P, HALVES, UNITS], U8, align_bytes=64)
+        nc.vector.quantize_mx(
+            out=ck_codes[:].rearrange("p h j -> p (h j)").bitcast(FP8X4),
+            scales=ck_scales[:].rearrange("p h j -> p (h j)"),
+            in_=ck_grouped[:].rearrange("p h j t -> p (h j t)"),
+        )
+        bias_t = psum_tr.tile([P, P], BF16, name="bias_t", tag="tr")
+        nc.tensor.transpose(bias_t[:], bias_rows[:], ident_bf[:])
+        bias_col = keep.tile([P, 1], F32)
+        nc.vector.tensor_copy(out=bias_col[:], in_=bias_t[:, 0:1])
+
+        old_part = []
+        one_minus_u = []
+        for c in range(PAIRS):
+            uh = keep.tile([P, BATCH, 2 * UNITS], F32, name="old_part%d" % c)
+            nc.gpsimd.tensor_tensor(out=uh[:], in0=u_sb[c][:], in1=h_sb[c][:], op=ALU.mult)
+            rest = keep.tile([P, BATCH, 2 * UNITS], F32, name="one_minus_u%d" % c)
+            nc.gpsimd.tensor_scalar(out=rest[:], in0=u_sb[c][:], scalar1=-1.0, scalar2=1.0, op0=ALU.mult, op1=ALU.add)
+            old_part.append(uh)
+            one_minus_u.append(rest)
+
+        for i in range(PAIRS + 2):
+            if 0 <= i - 2:
+                blend(i - 2)
+            if i + 1 < PAIRS:
+                transpose_adj(i + 1)
+            if i < PAIRS:
+                transpose_terms(i)
+            if 0 <= i - 1 < PAIRS:
+                candidate(i - 1)
+            if i + 1 < PAIRS:
+                diffuse(i + 1)

@@ -20,6 +20,8 @@ TERMS = 4
 HALVES = FEATS // P
 PASSES = NODES // (4 * P)
 PAIRS = NODES // (2 * P)
+RUN = 8
+RUNS = BATCH * FEATS // RUN
 FLOPS = 2 * NODES * NODES * BATCH * FEATS + 2 * BATCH * NODES * TERMS * FEATS * UNITS
 
 
@@ -32,6 +34,7 @@ def tile_gts_gcgrucell_pc_kernel(tc, adj, x0, x1, x2, u, h_prev, c_kernel, c_bia
     u_v = u.rearrange("b (c p e j) -> c p b (e j)", c=PAIRS, p=P, e=2, j=UNITS)
     h_v = h_prev.rearrange("b (c p e j) -> c p b (e j)", c=PAIRS, p=P, e=2, j=UNITS)
     out_v = out.rearrange("b (c p e j) -> c p b (e j)", c=PAIRS, p=P, e=2, j=UNITS)
+    ck_v = c_kernel.rearrange("(h B w e a s) j -> h a w B e (s j)", h=HALVES, B=P // RUN, w=RUN // 2, e=2, a=2, s=2)
 
     with ExitStack() as ctx:
         keep = ctx.enter_context(tc.tile_pool(name="keep", bufs=1))
@@ -45,11 +48,10 @@ def tile_gts_gcgrucell_pc_kernel(tc, adj, x0, x1, x2, u, h_prev, c_kernel, c_bia
         x2_sb = [keep.tile([P, BATCH, 4, FEATS], BF16, name="x2_%d" % g) for g in range(PASSES)]
         u_sb = [keep.tile([P, BATCH, 2 * UNITS], BF16, name="u%d" % c) for c in range(PAIRS)]
         h_sb = [keep.tile([P, BATCH, 2 * UNITS], BF16, name="h%d" % c) for c in range(PAIRS)]
-        ck_sb = keep.tile([P, HALVES, TERMS, UNITS], BF16)
+        ck_sb = keep.tile([P, HALVES, 2, 2 * UNITS], BF16)
         bias_rows = keep.tile([P, P], BF16)
 
         nc.vector.memset(bias_rows[:], 0.0)
-        nc.scalar.dma_start(out=ck_sb[:], in_=c_kernel.rearrange("(h p t) j -> p h (t j)", h=HALVES, p=P, t=TERMS))
         nc.scalar.dma_start(out=bias_rows[0:1, :], in_=c_bias.rearrange("(o j) -> o j", o=1))
 
         nc.sync.dma_start(out=adj_sb[0][:], in_=adj_v[0])
@@ -62,6 +64,11 @@ def tile_gts_gcgrucell_pc_kernel(tc, adj, x0, x1, x2, u, h_prev, c_kernel, c_bia
             nc.sync.dma_start(out=x0_sb[c][:], in_=x0_v[c])
             nc.sync.dma_start(out=u_sb[c][:], in_=u_v[c])
             nc.sync.dma_start(out=h_sb[c][:], in_=h_v[c])
+            if c == 0:
+                for a in range(2):
+                    for w in range(RUN // 2):
+                        for h in range(HALVES):
+                            nc.sync.dma_start(out=ck_sb[4 * a + w : P : RUN, h], in_=ck_v[h, a, w])
 
         ident_bf = keep.tile([P, P], BF16)
         make_identity(nc, ident_bf[:])
@@ -87,12 +94,19 @@ def tile_gts_gcgrucell_pc_kernel(tc, adj, x0, x1, x2, u, h_prev, c_kernel, c_bia
             x2_codes.append(codes)
             x2_scales.append(scales)
 
+        rows = [keep.tile([P, 2, 2, RUNS, 2, RUN], BF16, name="rows%d" % c) for c in range(PAIRS)]
+
         adj_codes = {}
         adj_scales = {}
-        x3_sb = {}
         xk_codes = {}
         xk_scales = {}
         cand_t = {}
+
+        def place_term(c, k, term):
+            nc.vector.tensor_copy(
+                out=rows[c][:, :, k % 2, :, k // 2, :].rearrange("p e (b x) i -> p e b x i", b=BATCH),
+                in_=term.rearrange("p b e (x i) -> p e b x i", i=RUN),
+            )
 
         def transpose_adj(c):
             grouped = work.tile([P, 2, PASSES, P, 2], F32, name="adj_grouped", align_bytes=64)
@@ -115,12 +129,11 @@ def tile_gts_gcgrucell_pc_kernel(tc, adj, x0, x1, x2, u, h_prev, c_kernel, c_bia
             adj_scales[c] = scales
 
         def diffuse(c):
-            x3 = work.tile([P, 2, BATCH, FEATS], BF16, name="x3")
             for e in range(2):
-                acc = psum_mx.tile([P, BATCH, FEATS], F32, name="acc1", tag="mx")
+                acc = psum_mx.tile([P, BATCH, FEATS // RUN, RUN], F32, name="acc1", tag="mx")
                 for g in range(PASSES):
                     nc.tensor.matmul_mx(
-                        out=acc[:].rearrange("p b f -> p (b f)"),
+                        out=acc[:].rearrange("p b x i -> p (b x i)"),
                         lhsT=adj_codes[c][:, e, g, :].bitcast(FP8X4),
                         lhsT_scale=adj_scales[c][:, e, g, :],
                         rhs=x2_codes[g][:].bitcast(FP8X4),
@@ -129,44 +142,35 @@ def tile_gts_gcgrucell_pc_kernel(tc, adj, x0, x1, x2, u, h_prev, c_kernel, c_bia
                         stop=(g == PASSES - 1),
                     )
                 nc.vector.scalar_tensor_tensor(
-                    out=x3[:, e],
+                    out=rows[c][:, e, 1, :, 1, :].rearrange("p (b x) i -> p b x i", b=BATCH),
                     in0=acc[:],
                     scalar=2.0,
-                    in1=x1_sb[c][:, :, e, :],
+                    in1=x1_sb[c][:, :, e, :].rearrange("p b (x i) -> p b x i", i=RUN),
                     op0=ALU.mult,
                     op1=ALU.subtract,
                 )
-            x3_sb[c] = x3
 
         def transpose_terms(c):
-            grouped = work.tile([P, BATCH, HALVES, 2 * P, TERMS], BF16, name="xk_grouped", align_bytes=64)
+            grouped = work.tile([P, BATCH, HALVES, 2 * P, 2], F32, name="xk_grouped", align_bytes=64)
             codes = work.tile([P, BATCH, HALVES, 2 * P], U32, name="xk_codes", align_bytes=64)
             scales = work.tile([P, BATCH, HALVES, 2 * P], U8, name="xk_scales", align_bytes=64)
             for b in range(BATCH):
                 for e in range(2):
-                    terms = [
-                        x0_sb[c][:, b, e, :],
-                        x1_sb[c][:, b, e, :],
-                        x2_sb[c // 2][:, b, 2 * (c % 2) + e, :],
-                        x3_sb[c][:, e, b, :],
-                    ]
-                    xk_t = psum_tr.tile([P, HALVES, TERMS, P], BF16, name="xk_t", tag="tr")
+                    xk_t = psum_tr.tile([P, HALVES, 2, P], F32, name="xk_t", tag="tr")
                     for h in range(HALVES):
-                        for k in range(TERMS):
-                            nc.tensor.transpose(xk_t[:, h, k, :], terms[k][:, h * P : (h + 1) * P], ident_bf[:])
-                    dst = grouped[:, b, :, e * P : (e + 1) * P, :]
-                    src = xk_t[:].rearrange("p h k n -> p h n k")
-                    if (b, e) == (1, 0):
-                        nc.vector.tensor_copy(out=dst, in_=src)
-                    else:
-                        nc.scalar.copy(out=dst, in_=src)
-                if b == 1:
-                    for bb in range(BATCH):
-                        nc.vector.quantize_mx(
-                            out=codes[:, bb].rearrange("p h n -> p (h n)").bitcast(FP8X4),
-                            scales=scales[:, bb].rearrange("p h n -> p (h n)"),
-                            in_=grouped[:, bb].rearrange("p h n k -> p (h n k)"),
-                        )
+                        first = (b * HALVES + h) * (P // RUN)
+                        for s in range(2):
+                            words = rows[c][:, e, s, first : first + P // RUN].rearrange("p x a i -> p (x a i)")
+                            nc.tensor.transpose(xk_t[:, h, s, :], words.bitcast(F32), ident_f32[:])
+                    nc.scalar.copy(
+                        out=grouped[:, b, :, e * P : (e + 1) * P, :],
+                        in_=xk_t[:].rearrange("p h s n -> p h n s"),
+                    )
+                nc.vector.quantize_mx(
+                    out=codes[:, b].rearrange("p h n -> p (h n)").bitcast(FP8X4),
+                    scales=scales[:, b].rearrange("p h n -> p (h n)"),
+                    in_=grouped[:, b].rearrange("p h n s -> p (h n s)").bitcast(BF16),
+                )
             xk_codes[c] = codes
             xk_scales[c] = scales
 
@@ -198,28 +202,35 @@ def tile_gts_gcgrucell_pc_kernel(tc, adj, x0, x1, x2, u, h_prev, c_kernel, c_bia
             for b in range(BATCH):
                 for e in range(2):
                     nc.tensor.transpose(cand_n[:, b, e, :], cand_t[c][:, b, e, :], ident_f32[:])
-            new_part = work.tile([P, BATCH, 2 * UNITS], F32, name="new_part")
-            nc.vector.tensor_tensor(
-                out=new_part[:].rearrange("p b x -> p (b x)"),
-                in0=cand_n[:].rearrange("p b e j -> p (b e j)"),
-                in1=one_minus_u[c][:].rearrange("p b x -> p (b x)"),
-                op=ALU.mult,
+            minus_new = work.tile([P, BATCH * 2 * UNITS], F32, name="minus_new")
+            nc.vector.scalar_tensor_tensor(
+                out=minus_new[:],
+                in0=u_sb[c][:].rearrange("p b x -> p (b x)"),
+                scalar=1.0,
+                in1=cand_n[:].rearrange("p b e j -> p (b e j)"),
+                op0=ALU.subtract,
+                op1=ALU.mult,
             )
             result = work.tile([P, BATCH, 2 * UNITS], F32, name="result")
-            nc.gpsimd.tensor_tensor(out=result[:], in0=new_part[:], in1=old_part[c][:], op=ALU.add)
+            nc.gpsimd.tensor_tensor(
+                out=result[:].rearrange("p b x -> p (b x)"), in0=old_part[c][:], in1=minus_new[:], op=ALU.subtract
+            )
             nc.sync.dma_start(out=out_v[c], in_=result[:])
 
         transpose_adj(0)
         diffuse(0)
 
-        ck_grouped = keep.tile([P, HALVES, UNITS, TERMS], BF16, align_bytes=64)
-        nc.vector.tensor_copy(out=ck_grouped[:], in_=ck_sb[:].rearrange("p h t j -> p h j t"))
+        ck_grouped = keep.tile([P, HALVES, UNITS, 2, 2], BF16, align_bytes=64)
+        for h in range(HALVES):
+            nc.vector.tensor_copy(
+                out=ck_grouped[:, h], in_=ck_sb[:, h].rearrange("p e (s j) -> p j s e", s=2)
+            )
         ck_codes = keep.tile([P, HALVES, UNITS], U32, align_bytes=64)
         ck_scales = keep.tile([P, HALVES, UNITS], U8, align_bytes=64)
         nc.vector.quantize_mx(
             out=ck_codes[:].rearrange("p h j -> p (h j)").bitcast(FP8X4),
             scales=ck_scales[:].rearrange("p h j -> p (h j)"),
-            in_=ck_grouped[:].rearrange("p h j t -> p (h j t)"),
+            in_=ck_grouped[:].rearrange("p h j s e -> p (h j s e)"),
         )
         bias_t = psum_tr.tile([P, P], BF16, name="bias_t", tag="tr")
         nc.tensor.transpose(bias_t[:], bias_rows[:], ident_bf[:])
@@ -227,14 +238,15 @@ def tile_gts_gcgrucell_pc_kernel(tc, adj, x0, x1, x2, u, h_prev, c_kernel, c_bia
         nc.vector.tensor_copy(out=bias_col[:], in_=bias_t[:, 0:1])
 
         old_part = []
-        one_minus_u = []
         for c in range(PAIRS):
-            uh = keep.tile([P, BATCH, 2 * UNITS], F32, name="old_part%d" % c)
-            nc.gpsimd.tensor_tensor(out=uh[:], in0=u_sb[c][:], in1=h_sb[c][:], op=ALU.mult)
-            rest = keep.tile([P, BATCH, 2 * UNITS], F32, name="one_minus_u%d" % c)
-            nc.gpsimd.tensor_scalar(out=rest[:], in0=u_sb[c][:], scalar1=-1.0, scalar2=1.0, op0=ALU.mult, op1=ALU.add)
+            uh = keep.tile([P, BATCH * 2 * UNITS], F32, name="old_part%d" % c)
+            nc.gpsimd.tensor_tensor(
+                out=uh[:],
+                in0=u_sb[c][:].rearrange("p b x -> p (b x)"),
+                in1=h_sb[c][:].rearrange("p b x -> p (b x)"),
+                op=ALU.mult,
+            )
             old_part.append(uh)
-            one_minus_u.append(rest)
 
         for i in range(PAIRS + 2):
             if 0 <= i - 2:
@@ -242,6 +254,9 @@ def tile_gts_gcgrucell_pc_kernel(tc, adj, x0, x1, x2, u, h_prev, c_kernel, c_bia
             if i + 1 < PAIRS:
                 transpose_adj(i + 1)
             if i < PAIRS:
+                place_term(i, 2, x2_sb[i // 2][:, :, 2 * (i % 2) : 2 * (i % 2) + 2, :])
+                place_term(i, 1, x1_sb[i][:])
+                place_term(i, 0, x0_sb[i][:])
                 transpose_terms(i)
             if 0 <= i - 1 < PAIRS:
                 candidate(i - 1)

@@ -34,21 +34,21 @@ def tile_gts_gcgrucell_pc_kernel(tc, adj, x0, x1, x2, u, h_prev, c_kernel, c_bia
     u_v = u.rearrange("b (c p e j) -> c p b (e j)", c=PAIRS, p=P, e=2, j=UNITS)
     h_v = h_prev.rearrange("b (c p e j) -> c p b (e j)", c=PAIRS, p=P, e=2, j=UNITS)
     out_v = out.rearrange("b (c p e j) -> c p b (e j)", c=PAIRS, p=P, e=2, j=UNITS)
-    ck_v = c_kernel.rearrange("(h B w e a s) j -> h a w B e (s j)", h=HALVES, B=P // RUN, w=RUN // 2, e=2, a=2, s=2)
 
     with ExitStack() as ctx:
         keep = ctx.enter_context(tc.tile_pool(name="keep", bufs=1))
         work = ctx.enter_context(tc.tile_pool(name="work", bufs=2))
         psum_tr = ctx.enter_context(tc.psum_pool(name="psum_tr", bufs=5))
         psum_mx = ctx.enter_context(tc.psum_pool(name="psum_mx", bufs=3))
+        ctx.enter_context(tc.manual_schedule())
 
         adj_sb = [keep.tile([P, 2, NODES], BF16, name="adj%d" % c) for c in range(PAIRS)]
         x0_sb = [keep.tile([P, BATCH, 2, FEATS], BF16, name="x0_%d" % c) for c in range(PAIRS)]
         x1_sb = [keep.tile([P, BATCH, 2, FEATS], BF16, name="x1_%d" % c) for c in range(PAIRS)]
         x2_sb = [keep.tile([P, BATCH, 4, FEATS], BF16, name="x2_%d" % g) for g in range(PASSES)]
-        u_sb = [keep.tile([P, BATCH, 2 * UNITS], BF16, name="u%d" % c) for c in range(PAIRS)]
-        h_sb = [keep.tile([P, BATCH, 2 * UNITS], BF16, name="h%d" % c) for c in range(PAIRS)]
-        ck_sb = keep.tile([P, HALVES, 2, 2 * UNITS], BF16)
+        u_sb = [keep.tile([P, BATCH * 2 * UNITS], BF16, name="u%d" % c) for c in range(PAIRS)]
+        h_sb = [keep.tile([P, BATCH * 2 * UNITS], BF16, name="h%d" % c) for c in range(PAIRS)]
+        ck_sb = keep.tile([P, HALVES, TERMS, UNITS], BF16)
         bias_rows = keep.tile([P, P], BF16)
 
         nc.vector.memset(bias_rows[:], 0.0)
@@ -57,52 +57,71 @@ def tile_gts_gcgrucell_pc_kernel(tc, adj, x0, x1, x2, u, h_prev, c_kernel, c_bia
         nc.sync.dma_start(out=adj_sb[0][:], in_=adj_v[0])
         for c in range(PAIRS):
             nc.sync.dma_start(out=x2_sb[c // 2][:, :, 2 * (c % 2) : 2 * (c % 2) + 2, :], in_=x2_v[c])
-        for c in range(PAIRS):
-            if c > 0:
-                nc.sync.dma_start(out=adj_sb[c][:], in_=adj_v[c])
-            nc.sync.dma_start(out=x1_sb[c][:], in_=x1_v[c])
-            nc.sync.dma_start(out=x0_sb[c][:], in_=x0_v[c])
-            nc.sync.dma_start(out=u_sb[c][:], in_=u_v[c])
-            nc.sync.dma_start(out=h_sb[c][:], in_=h_v[c])
-            if c == 0:
-                for a in range(2):
-                    for w in range(RUN // 2):
-                        for h in range(HALVES):
-                            nc.sync.dma_start(out=ck_sb[4 * a + w : P : RUN, h], in_=ck_v[h, a, w])
+        nc.sync.dma_start(out=ck_sb[:], in_=c_kernel.rearrange("(h p k) j -> p h (k j)", h=HALVES, p=P, k=TERMS))
+        for c in range(PAIRS + 2):
+            if c + 1 < PAIRS:
+                nc.sync.dma_start(out=adj_sb[c + 1][:], in_=adj_v[c + 1])
+            if c < PAIRS:
+                nc.sync.dma_start(out=x1_sb[c][:], in_=x1_v[c])
+                nc.sync.dma_start(out=x0_sb[c][:], in_=x0_v[c])
+            if c >= 2:
+                nc.sync.dma_start(out=u_sb[c - 2][:].rearrange("p (b x) -> p b x", b=BATCH), in_=u_v[c - 2])
+                nc.sync.dma_start(out=h_sb[c - 2][:].rearrange("p (b x) -> p b x", b=BATCH), in_=h_v[c - 2])
 
-        ident_bf = keep.tile([P, P], BF16)
-        make_identity(nc, ident_bf[:])
         ident_f32 = keep.tile([P, P], F32)
         make_identity(nc, ident_f32[:])
+        ident_bf = keep.tile([P, P], BF16)
+        make_identity(nc, ident_bf[:])
         warm = keep.tile([P, 1], F32)
         nc.vector.memset(warm[:], 0.0)
         nc.scalar.activation(out=warm[:], in_=warm[:], func=ACT.Tanh)
+        move_rows = keep.tile([P, 2, 2, P], BF16)
+        nc.vector.memset(move_rows[:], 0.0)
+        for e in range(2):
+            for a in range(2):
+                nc.vector.tensor_copy(
+                    out=move_rows[:, e, a, :].rearrange("p (B x w) -> p B x w", x=2, w=RUN // 2)[:, :, a, :],
+                    in_=ident_bf[:].rearrange("p (B w y) -> p B w y", w=RUN // 2, y=2)[:, :, :, e],
+                )
 
-        x2_codes = []
-        x2_scales = []
-        for g in range(PASSES):
-            x2_grouped = keep.tile([P, BATCH, FEATS, 4], BF16, name="x2_grouped%d" % g, align_bytes=64)
-            nc.vector.tensor_copy(out=x2_grouped[:, 0], in_=x2_sb[g][:, 0].rearrange("p t f -> p f t"))
-            nc.scalar.copy(out=x2_grouped[:, 1], in_=x2_sb[g][:, 1].rearrange("p t f -> p f t"))
-            codes = keep.tile([P, BATCH * FEATS], U32, name="x2_codes%d" % g, align_bytes=64)
-            scales = keep.tile([P, BATCH * FEATS], U8, name="x2_scales%d" % g, align_bytes=64)
-            nc.vector.quantize_mx(
-                out=codes[:].bitcast(FP8X4),
-                scales=scales[:],
-                in_=x2_grouped[:].rearrange("p b f t -> p (b f t)"),
-            )
-            x2_codes.append(codes)
-            x2_scales.append(scales)
-
+        x2_grouped = [keep.tile([P, BATCH, FEATS, 4], BF16, name="x2_grouped%d" % g, align_bytes=64) for g in range(PASSES)]
+        x2_codes = [keep.tile([P, BATCH * FEATS], U32, name="x2_codes%d" % g, align_bytes=64) for g in range(PASSES)]
+        x2_scales = [keep.tile([P, BATCH * FEATS], U8, name="x2_scales%d" % g, align_bytes=64) for g in range(PASSES)]
         rows = [keep.tile([P, 2, 2, RUNS, 2, RUN], BF16, name="rows%d" % c) for c in range(PAIRS)]
+        old_part = [keep.tile([P, BATCH * 2 * UNITS], F32, name="old_part%d" % c) for c in range(PAIRS)]
+        ck_grouped = keep.tile([P, HALVES, UNITS, 2, 2], BF16, align_bytes=64)
+        ck_codes = keep.tile([P, HALVES, UNITS], U32, align_bytes=64)
+        ck_scales = keep.tile([P, HALVES, UNITS], U8, align_bytes=64)
+        bias_col = keep.tile([P, 1], F32)
 
+        adj_grouped = {}
         adj_codes = {}
         adj_scales = {}
+        acc1 = {}
+        xk_grouped = {}
         xk_codes = {}
         xk_scales = {}
         cand_t = {}
+        cand_n = {}
 
-        def place_term(c, k, term):
+        def regroup_x2(g):
+            nc.vector.tensor_copy(out=x2_grouped[g][:, 0], in_=x2_sb[g][:, 0].rearrange("p t f -> p f t"))
+            nc.scalar.copy(out=x2_grouped[g][:, 1], in_=x2_sb[g][:, 1].rearrange("p t f -> p f t"))
+
+        def quantise_x2(g):
+            nc.vector.quantize_mx(
+                out=x2_codes[g][:].bitcast(FP8X4),
+                scales=x2_scales[g][:],
+                in_=x2_grouped[g][:].rearrange("p b f t -> p (b f t)"),
+            )
+
+        def place_term(c, k):
+            if k == 2:
+                term = x2_sb[c // 2][:, :, 2 * (c % 2) : 2 * (c % 2) + 2, :]
+            elif k == 1:
+                term = x1_sb[c][:]
+            else:
+                term = x0_sb[c][:]
             nc.vector.tensor_copy(
                 out=rows[c][:, :, k % 2, :, k // 2, :].rearrange("p e (b x) i -> p e b x i", b=BATCH),
                 in_=term.rearrange("p b e (x i) -> p e b x i", i=RUN),
@@ -118,12 +137,15 @@ def tile_gts_gcgrucell_pc_kernel(tc, adj, x0, x1, x2, u, h_prev, c_kernel, c_bia
                         first = (2 * g + w) * P
                         nc.tensor.transpose(adj_t[:, g, w, :], words[:, first : first + P], ident_f32[:])
                 nc.scalar.copy(out=grouped[:, e], in_=adj_t[:].rearrange("p g w n -> p g n w"))
+            adj_grouped[c] = grouped
+
+        def quantise_adj(c):
             codes = work.tile([P, 2, PASSES, P], U32, name="adj_codes", align_bytes=64)
             scales = work.tile([P, 2, PASSES, P], U8, name="adj_scales", align_bytes=64)
             nc.vector.quantize_mx(
                 out=codes[:].rearrange("p e g n -> p (e g n)").bitcast(FP8X4),
                 scales=scales[:].rearrange("p e g n -> p (e g n)"),
-                in_=grouped[:].rearrange("p e g n w -> p (e g n w)").bitcast(BF16),
+                in_=adj_grouped[c][:].rearrange("p e g n w -> p (e g n w)").bitcast(BF16),
             )
             adj_codes[c] = codes
             adj_scales[c] = scales
@@ -141,9 +163,13 @@ def tile_gts_gcgrucell_pc_kernel(tc, adj, x0, x1, x2, u, h_prev, c_kernel, c_bia
                         start=(g == 0),
                         stop=(g == PASSES - 1),
                     )
+                acc1[(c, e)] = acc
+
+        def third_term(c):
+            for e in range(2):
                 nc.vector.scalar_tensor_tensor(
                     out=rows[c][:, e, 1, :, 1, :].rearrange("p (b x) i -> p b x i", b=BATCH),
-                    in0=acc[:],
+                    in0=acc1[(c, e)][:],
                     scalar=2.0,
                     in1=x1_sb[c][:, :, e, :].rearrange("p b (x i) -> p b x i", i=RUN),
                     op0=ALU.mult,
@@ -152,8 +178,6 @@ def tile_gts_gcgrucell_pc_kernel(tc, adj, x0, x1, x2, u, h_prev, c_kernel, c_bia
 
         def transpose_terms(c):
             grouped = work.tile([P, BATCH, HALVES, 2 * P, 2], F32, name="xk_grouped", align_bytes=64)
-            codes = work.tile([P, BATCH, HALVES, 2 * P], U32, name="xk_codes", align_bytes=64)
-            scales = work.tile([P, BATCH, HALVES, 2 * P], U8, name="xk_scales", align_bytes=64)
             for b in range(BATCH):
                 for e in range(2):
                     xk_t = psum_tr.tile([P, HALVES, 2, P], F32, name="xk_t", tag="tr")
@@ -166,13 +190,16 @@ def tile_gts_gcgrucell_pc_kernel(tc, adj, x0, x1, x2, u, h_prev, c_kernel, c_bia
                         out=grouped[:, b, :, e * P : (e + 1) * P, :],
                         in_=xk_t[:].rearrange("p h s n -> p h n s"),
                     )
-                nc.vector.quantize_mx(
-                    out=codes[:, b].rearrange("p h n -> p (h n)").bitcast(FP8X4),
-                    scales=scales[:, b].rearrange("p h n -> p (h n)"),
-                    in_=grouped[:, b].rearrange("p h n s -> p (h n s)").bitcast(BF16),
-                )
-            xk_codes[c] = codes
-            xk_scales[c] = scales
+            xk_grouped[c] = grouped
+            xk_codes[c] = work.tile([P, BATCH, HALVES, 2 * P], U32, name="xk_codes", align_bytes=64)
+            xk_scales[c] = work.tile([P, BATCH, HALVES, 2 * P], U8, name="xk_scales", align_bytes=64)
+
+        def quantise_terms(c, b):
+            nc.vector.quantize_mx(
+                out=xk_codes[c][:, b].rearrange("p h n -> p (h n)").bitcast(FP8X4),
+                scales=xk_scales[c][:, b].rearrange("p h n -> p (h n)"),
+                in_=xk_grouped[c][:, b].rearrange("p h n s -> p (h n s)").bitcast(BF16),
+            )
 
         def candidate(c):
             acc = psum_mx.tile([P, BATCH, 2 * P], F32, name="acc2", tag="mx")
@@ -197,68 +224,77 @@ def tile_gts_gcgrucell_pc_kernel(tc, adj, x0, x1, x2, u, h_prev, c_kernel, c_bia
             )
             cand_t[c] = cand
 
-        def blend(c):
-            cand_n = psum_tr.tile([P, BATCH, 2, UNITS], F32, name="cand_n", tag="tr")
+        def transpose_candidate(c):
+            back = psum_tr.tile([P, BATCH, 2, UNITS], F32, name="cand_n", tag="tr")
             for b in range(BATCH):
                 for e in range(2):
-                    nc.tensor.transpose(cand_n[:, b, e, :], cand_t[c][:, b, e, :], ident_f32[:])
+                    nc.tensor.transpose(back[:, b, e, :], cand_t[c][:, b, e, :], ident_f32[:])
+            cand_n[c] = back
+
+        def blend(c):
             minus_new = work.tile([P, BATCH * 2 * UNITS], F32, name="minus_new")
             nc.vector.scalar_tensor_tensor(
                 out=minus_new[:],
-                in0=u_sb[c][:].rearrange("p b x -> p (b x)"),
+                in0=u_sb[c][:],
                 scalar=1.0,
-                in1=cand_n[:].rearrange("p b e j -> p (b e j)"),
+                in1=cand_n[c][:].rearrange("p b e j -> p (b e j)"),
                 op0=ALU.subtract,
                 op1=ALU.mult,
             )
-            result = work.tile([P, BATCH, 2 * UNITS], F32, name="result")
-            nc.gpsimd.tensor_tensor(
-                out=result[:].rearrange("p b x -> p (b x)"), in0=old_part[c][:], in1=minus_new[:], op=ALU.subtract
-            )
-            nc.sync.dma_start(out=out_v[c], in_=result[:])
+            result = work.tile([P, BATCH * 2 * UNITS], F32, name="result")
+            nc.vector.tensor_tensor(out=result[:], in0=old_part[c][:], in1=minus_new[:], op=ALU.subtract)
+            nc.sync.dma_start(out=out_v[c], in_=result[:].rearrange("p (b x) -> p b x", b=BATCH))
 
         transpose_adj(0)
-        diffuse(0)
-
-        ck_grouped = keep.tile([P, HALVES, UNITS, 2, 2], BF16, align_bytes=64)
+        regroup_x2(0)
+        quantise_adj(0)
+        quantise_x2(0)
+        regroup_x2(1)
         for h in range(HALVES):
-            nc.vector.tensor_copy(
-                out=ck_grouped[:, h], in_=ck_sb[:, h].rearrange("p e (s j) -> p j s e", s=2)
-            )
-        ck_codes = keep.tile([P, HALVES, UNITS], U32, align_bytes=64)
-        ck_scales = keep.tile([P, HALVES, UNITS], U8, align_bytes=64)
+            ck_moved = psum_tr.tile([P, 2, 2 * UNITS], F32, name="ck_moved", tag="tr")
+            for e in range(2):
+                for a in range(2):
+                    nc.tensor.matmul(
+                        out=ck_moved[:, e, :],
+                        lhsT=move_rows[:, e, a, :],
+                        rhs=ck_sb[:, h, 2 * a : 2 * a + 2, :].rearrange("p s j -> p (s j)"),
+                        start=(a == 0),
+                        stop=(a == 1),
+                    )
+            nc.scalar.copy(out=ck_grouped[:, h], in_=ck_moved[:].rearrange("p e (s j) -> p j s e", s=2))
+        bias_t = psum_tr.tile([P, P], BF16, name="bias_t", tag="tr")
+        nc.tensor.transpose(bias_t[:], bias_rows[:], ident_bf[:])
+        quantise_x2(1)
+        diffuse(0)
+        transpose_adj(1)
+        place_term(0, 2)
         nc.vector.quantize_mx(
             out=ck_codes[:].rearrange("p h j -> p (h j)").bitcast(FP8X4),
             scales=ck_scales[:].rearrange("p h j -> p (h j)"),
             in_=ck_grouped[:].rearrange("p h j s e -> p (h j s e)"),
         )
-        bias_t = psum_tr.tile([P, P], BF16, name="bias_t", tag="tr")
-        nc.tensor.transpose(bias_t[:], bias_rows[:], ident_bf[:])
-        bias_col = keep.tile([P, 1], F32)
+        place_term(0, 1)
+        place_term(0, 0)
         nc.vector.tensor_copy(out=bias_col[:], in_=bias_t[:, 0:1])
 
-        old_part = []
-        for c in range(PAIRS):
-            uh = keep.tile([P, BATCH * 2 * UNITS], F32, name="old_part%d" % c)
-            nc.gpsimd.tensor_tensor(
-                out=uh[:],
-                in0=u_sb[c][:].rearrange("p b x -> p (b x)"),
-                in1=h_sb[c][:].rearrange("p b x -> p (b x)"),
-                op=ALU.mult,
-            )
-            old_part.append(uh)
-
-        for i in range(PAIRS + 2):
-            if 0 <= i - 2:
-                blend(i - 2)
+        for i in range(-1, PAIRS + 1):
+            if 0 <= i - 1:
+                transpose_candidate(i - 1)
+            if i + 3 < PAIRS:
+                transpose_adj(i + 3)
             if i + 1 < PAIRS:
-                transpose_adj(i + 1)
-            if i < PAIRS:
-                place_term(i, 2, x2_sb[i // 2][:, :, 2 * (i % 2) : 2 * (i % 2) + 2, :])
-                place_term(i, 1, x1_sb[i][:])
-                place_term(i, 0, x0_sb[i][:])
-                transpose_terms(i)
-            if 0 <= i - 1 < PAIRS:
-                candidate(i - 1)
-            if i + 1 < PAIRS:
-                diffuse(i + 1)
+                third_term(i + 1)
+                transpose_terms(i + 1)
+            if i + 2 < PAIRS:
+                quantise_adj(i + 2)
+                place_term(i + 2, 2)
+                place_term(i + 2, 1)
+                place_term(i + 2, 0)
+                diffuse(i + 2)
+            if 0 <= i < PAIRS:
+                quantise_terms(i, 0)
+                quantise_terms(i, 1)
+                candidate(i)
+                nc.vector.tensor_tensor(out=old_part[i][:], in0=u_sb[i][:], in1=h_sb[i][:], op=ALU.mult)
+            if 0 <= i - 1:
+                blend(i - 1)

@@ -247,6 +247,8 @@ def tile_gts_gcgrucell_pc_kernel(tc, adj, x0, x1, x2, u, h_prev, c_kernel, c_bia
 
         transpose_adj(0)
         regroup_x2(0)
+        place_term(0, 2)
+        place_term(1, 2)
         quantise_adj(0)
         quantise_x2(0)
         regroup_x2(1)
@@ -264,10 +266,11 @@ def tile_gts_gcgrucell_pc_kernel(tc, adj, x0, x1, x2, u, h_prev, c_kernel, c_bia
             nc.scalar.copy(out=ck_grouped[:, h], in_=ck_moved[:].rearrange("p e (s j) -> p j s e", s=2))
         bias_t = psum_tr.tile([P, P], BF16, name="bias_t", tag="tr")
         nc.tensor.transpose(bias_t[:], bias_rows[:], ident_bf[:])
+        transpose_adj(1)
+        place_term(2, 2)
+        place_term(3, 2)
         quantise_x2(1)
         diffuse(0)
-        transpose_adj(1)
-        place_term(0, 2)
         nc.vector.quantize_mx(
             out=ck_codes[:].rearrange("p h j -> p (h j)").bitcast(FP8X4),
             scales=ck_scales[:].rearrange("p h j -> p (h j)"),
@@ -277,24 +280,24 @@ def tile_gts_gcgrucell_pc_kernel(tc, adj, x0, x1, x2, u, h_prev, c_kernel, c_bia
         place_term(0, 0)
         nc.vector.tensor_copy(out=bias_col[:], in_=bias_t[:, 0:1])
 
-        for i in range(-1, PAIRS + 1):
-            if 0 <= i - 1:
-                transpose_candidate(i - 1)
+        for i in range(-1, PAIRS + 2):
+            if 0 <= i - 2:
+                transpose_candidate(i - 2)
             if i + 3 < PAIRS:
                 transpose_adj(i + 3)
+            if i + 2 < PAIRS:
+                quantise_adj(i + 2)
+                diffuse(i + 2)
             if i + 1 < PAIRS:
                 third_term(i + 1)
                 transpose_terms(i + 1)
             if i + 2 < PAIRS:
-                quantise_adj(i + 2)
-                place_term(i + 2, 2)
                 place_term(i + 2, 1)
                 place_term(i + 2, 0)
-                diffuse(i + 2)
             if 0 <= i < PAIRS:
                 quantise_terms(i, 0)
                 quantise_terms(i, 1)
                 candidate(i)
                 nc.vector.tensor_tensor(out=old_part[i][:], in0=u_sb[i][:], in1=h_sb[i][:], op=ALU.mult)
-            if 0 <= i - 1:
-                blend(i - 1)
+            if 0 <= i - 2:
+                blend(i - 2)

@@ -72,6 +72,8 @@ def tile_gts_gcgrucell_pc_kernel(tc, adj, x0, x1, x2, u, h_prev, c_kernel, c_bia
         make_identity(nc, ident_f32[:])
         ident_bf = keep.tile([P, P], BF16)
         make_identity(nc, ident_bf[:])
+        minus_ident = keep.tile([P, P], BF16)
+        nc.vector.tensor_scalar(out=minus_ident[:], in0=ident_bf[:], scalar1=-1.0, scalar2=None, op0=ALU.mult)
         warm = keep.tile([P, 1], F32)
         nc.vector.memset(warm[:], 0.0)
         nc.scalar.activation(out=warm[:], in_=warm[:], func=ACT.Tanh)
@@ -88,7 +90,6 @@ def tile_gts_gcgrucell_pc_kernel(tc, adj, x0, x1, x2, u, h_prev, c_kernel, c_bia
         x2_codes = [keep.tile([P, BATCH * FEATS], U32, name="x2_codes%d" % g, align_bytes=64) for g in range(PASSES)]
         x2_scales = [keep.tile([P, BATCH * FEATS], U8, name="x2_scales%d" % g, align_bytes=64) for g in range(PASSES)]
         rows = [keep.tile([P, 2, 2, RUNS, 2, RUN], BF16, name="rows%d" % c) for c in range(PAIRS)]
-        old_part = [keep.tile([P, BATCH * 2 * UNITS], F32, name="old_part%d" % c) for c in range(PAIRS)]
         ck_grouped = keep.tile([P, HALVES, UNITS, 2, 2], BF16, align_bytes=64)
         ck_codes = keep.tile([P, HALVES, UNITS], U32, align_bytes=64)
         ck_scales = keep.tile([P, HALVES, UNITS], U8, align_bytes=64)
@@ -226,9 +227,23 @@ def tile_gts_gcgrucell_pc_kernel(tc, adj, x0, x1, x2, u, h_prev, c_kernel, c_bia
 
         def transpose_candidate(c):
             back = psum_tr.tile([P, BATCH, 2, UNITS], F32, name="cand_n", tag="tr")
+            nc.tensor.matmul(
+                out=back[:].rearrange("p b e j -> p (b e j)"),
+                lhsT=minus_ident[:],
+                rhs=h_sb[c][:],
+                start=True,
+                stop=False,
+            )
             for b in range(BATCH):
                 for e in range(2):
-                    nc.tensor.transpose(back[:, b, e, :], cand_t[c][:, b, e, :], ident_f32[:])
+                    nc.tensor.matmul(
+                        out=back[:, b, e, :],
+                        lhsT=cand_t[c][:, b, e, :],
+                        rhs=ident_f32[:],
+                        is_transpose=True,
+                        start=False,
+                        stop=(b == BATCH - 1 and e == 1),
+                    )
             cand_n[c] = back
 
         def blend(c):
@@ -242,7 +257,7 @@ def tile_gts_gcgrucell_pc_kernel(tc, adj, x0, x1, x2, u, h_prev, c_kernel, c_bia
                 op1=ALU.mult,
             )
             result = work.tile([P, BATCH * 2 * UNITS], F32, name="result")
-            nc.vector.tensor_tensor(out=result[:], in0=old_part[c][:], in1=minus_new[:], op=ALU.subtract)
+            nc.vector.tensor_tensor(out=result[:], in0=h_sb[c][:], in1=minus_new[:], op=ALU.subtract)
             nc.sync.dma_start(out=out_v[c], in_=result[:].rearrange("p (b x) -> p b x", b=BATCH))
 
         transpose_adj(0)
@@ -298,6 +313,5 @@ def tile_gts_gcgrucell_pc_kernel(tc, adj, x0, x1, x2, u, h_prev, c_kernel, c_bia
                 quantise_terms(i, 0)
                 quantise_terms(i, 1)
                 candidate(i)
-                nc.vector.tensor_tensor(out=old_part[i][:], in0=u_sb[i][:], in1=h_sb[i][:], op=ALU.mult)
             if 0 <= i - 2:
                 blend(i - 2)

@@ -30,7 +30,7 @@ def tile_gts_gcgrucell_pc_kernel(tc, adj, x0, x1, x2, u, h_prev, c_kernel, c_bia
     adj_v = adj.rearrange("(c p e) m -> c p (e m)", c=PAIRS, p=P, e=2)
     x0_v = x0.rearrange("b (c p e) f -> c p b (e f)", c=PAIRS, p=P, e=2)
     x1_v = x1.rearrange("b (c p e) f -> c p b (e f)", c=PAIRS, p=P, e=2)
-    x2_v = x2.rearrange("b (c p e) f -> c p b (e f)", c=PAIRS, p=P, e=2)
+    x2_v = x2.rearrange("b (g w p e) f -> g b p w (e f)", g=PASSES, w=2, p=P, e=2)
     u_v = u.rearrange("b (c p e j) -> c p b (e j)", c=PAIRS, p=P, e=2, j=UNITS)
     h_v = h_prev.rearrange("b (c p e j) -> c p b (e j)", c=PAIRS, p=P, e=2, j=UNITS)
     out_v = out.rearrange("b (c p e j) -> c p b (e j)", c=PAIRS, p=P, e=2, j=UNITS)
@@ -54,15 +54,18 @@ def tile_gts_gcgrucell_pc_kernel(tc, adj, x0, x1, x2, u, h_prev, c_kernel, c_bia
         nc.vector.memset(bias_rows[:], 0.0)
         nc.scalar.dma_start(out=bias_rows[0:1, :], in_=c_bias.rearrange("(o j) -> o j", o=1))
 
-        nc.sync.dma_start(out=adj_sb[0][:], in_=adj_v[0])
-        for c in range(PAIRS):
-            nc.sync.dma_start(out=x2_sb[c // 2][:, :, 2 * (c % 2) : 2 * (c % 2) + 2, :], in_=x2_v[c])
+        for g in range(PASSES):
+            for b in range(BATCH):
+                nc.sync.dma_start(out=x2_sb[g][:, b].rearrange("p (w e) f -> p w (e f)", e=2), in_=x2_v[g, b])
+        for e in range(2):
+            nc.sync.dma_start(out=adj_sb[0][:, e, :], in_=adj_v[0][:, e * NODES : (e + 1) * NODES])
         nc.sync.dma_start(out=ck_sb[:], in_=c_kernel.rearrange("(h p k) j -> p h (k j)", h=HALVES, p=P, k=TERMS))
         for c in range(PAIRS + 2):
+            if c < PAIRS:
+                nc.sync.dma_start(out=x1_sb[c][:], in_=x1_v[c])
             if c + 1 < PAIRS:
                 nc.sync.dma_start(out=adj_sb[c + 1][:], in_=adj_v[c + 1])
             if c < PAIRS:
-                nc.sync.dma_start(out=x1_sb[c][:], in_=x1_v[c])
                 nc.sync.dma_start(out=x0_sb[c][:], in_=x0_v[c])
             if c >= 2:
                 nc.sync.dma_start(out=u_sb[c - 2][:].rearrange("p (b x) -> p b x", b=BATCH), in_=u_v[c - 2])
@@ -103,11 +106,37 @@ def tile_gts_gcgrucell_pc_kernel(tc, adj, x0, x1, x2, u, h_prev, c_kernel, c_bia
         xk_codes = {}
         xk_scales = {}
         cand_t = {}
+        acc2 = {}
         cand_n = {}
+        minus_new = {}
 
-        def regroup_x2(g):
-            nc.vector.tensor_copy(out=x2_grouped[g][:, 0], in_=x2_sb[g][:, 0].rearrange("p t f -> p f t"))
-            nc.scalar.copy(out=x2_grouped[g][:, 1], in_=x2_sb[g][:, 1].rearrange("p t f -> p f t"))
+        def move_ck(h):
+            ck_moved = psum_tr.tile([P, 2, 2 * UNITS], F32, name="ck_moved", tag="tr")
+            for e in range(2):
+                for a in range(2):
+                    nc.tensor.matmul(
+                        out=ck_moved[:, e, :],
+                        lhsT=move_rows[:, e, a, :],
+                        rhs=ck_sb[:, h, 2 * a : 2 * a + 2, :].rearrange("p s j -> p (s j)"),
+                        start=(a == 0),
+                        stop=(a == 1),
+                    )
+            nc.scalar.copy(out=ck_grouped[:, h], in_=ck_moved[:].rearrange("p e (s j) -> p j s e", s=2))
+
+        def quantise_ck():
+            nc.vector.quantize_mx(
+                out=ck_codes[:].rearrange("p h j -> p (h j)").bitcast(FP8X4),
+                scales=ck_scales[:].rearrange("p h j -> p (h j)"),
+                in_=ck_grouped[:].rearrange("p h j s e -> p (h j s e)"),
+            )
+
+        def move_bias():
+            bias_t = psum_tr.tile([P, P], BF16, name="bias_t", tag="tr")
+            nc.tensor.transpose(bias_t[:], bias_rows[:], ident_bf[:])
+            return bias_t
+
+        def regroup_x2(g, b, copy):
+            copy(out=x2_grouped[g][:, b], in_=x2_sb[g][:, b].rearrange("p t f -> p f t"))
 
         def quantise_x2(g):
             nc.vector.quantize_mx(
@@ -116,114 +145,109 @@ def tile_gts_gcgrucell_pc_kernel(tc, adj, x0, x1, x2, u, h_prev, c_kernel, c_bia
                 in_=x2_grouped[g][:].rearrange("p b f t -> p (b f t)"),
             )
 
-        def place_term(c, k):
+        def place_term(c, k, copy=nc.vector.tensor_copy):
             if k == 2:
                 term = x2_sb[c // 2][:, :, 2 * (c % 2) : 2 * (c % 2) + 2, :]
             elif k == 1:
                 term = x1_sb[c][:]
             else:
                 term = x0_sb[c][:]
-            nc.vector.tensor_copy(
+            copy(
                 out=rows[c][:, :, k % 2, :, k // 2, :].rearrange("p e (b x) i -> p e b x i", b=BATCH),
                 in_=term.rearrange("p b e (x i) -> p e b x i", i=RUN),
             )
 
-        def transpose_adj(c):
-            grouped = work.tile([P, 2, PASSES, P, 2], F32, name="adj_grouped", align_bytes=64)
-            for e in range(2):
-                words = adj_sb[c][:, e, :].bitcast(F32)
-                adj_t = psum_tr.tile([P, PASSES, 2, P], F32, name="adj_t", tag="tr")
-                for g in range(PASSES):
-                    for w in range(2):
-                        first = (2 * g + w) * P
-                        nc.tensor.transpose(adj_t[:, g, w, :], words[:, first : first + P], ident_f32[:])
-                nc.scalar.copy(out=grouped[:, e], in_=adj_t[:].rearrange("p g w n -> p g n w"))
-            adj_grouped[c] = grouped
+        def transpose_adj(c, e):
+            if e == 0:
+                adj_grouped[c] = work.tile([P, 2, PASSES, P, 2], F32, name="adj_grouped", align_bytes=64)
+            words = adj_sb[c][:, e, :].bitcast(F32)
+            adj_t = psum_tr.tile([P, PASSES, 2, P], F32, name="adj_t", tag="tr")
+            for g in range(PASSES):
+                for w in range(2):
+                    first = (2 * g + w) * P
+                    nc.tensor.transpose(adj_t[:, g, w, :], words[:, first : first + P], ident_f32[:])
+            nc.scalar.copy(out=adj_grouped[c][:, e], in_=adj_t[:].rearrange("p g w n -> p g n w"))
 
-        def quantise_adj(c):
-            codes = work.tile([P, 2, PASSES, P], U32, name="adj_codes", align_bytes=64)
-            scales = work.tile([P, 2, PASSES, P], U8, name="adj_scales", align_bytes=64)
+        def quantise_adj(c, tiles=slice(0, 2)):
+            if c not in adj_codes:
+                adj_codes[c] = work.tile([P, 2, PASSES, P], U32, name="adj_codes", align_bytes=64)
+                adj_scales[c] = work.tile([P, 2, PASSES, P], U8, name="adj_scales", align_bytes=64)
             nc.vector.quantize_mx(
-                out=codes[:].rearrange("p e g n -> p (e g n)").bitcast(FP8X4),
-                scales=scales[:].rearrange("p e g n -> p (e g n)"),
-                in_=adj_grouped[c][:].rearrange("p e g n w -> p (e g n w)").bitcast(BF16),
+                out=adj_codes[c][:, tiles].rearrange("p e g n -> p (e g n)").bitcast(FP8X4),
+                scales=adj_scales[c][:, tiles].rearrange("p e g n -> p (e g n)"),
+                in_=adj_grouped[c][:, tiles].rearrange("p e g n w -> p (e g n w)").bitcast(BF16),
             )
-            adj_codes[c] = codes
-            adj_scales[c] = scales
 
-        def diffuse(c):
-            for e in range(2):
-                acc = psum_mx.tile([P, BATCH, FEATS // RUN, RUN], F32, name="acc1", tag="mx")
-                for g in range(PASSES):
-                    nc.tensor.matmul_mx(
-                        out=acc[:].rearrange("p b x i -> p (b x i)"),
-                        lhsT=adj_codes[c][:, e, g, :].bitcast(FP8X4),
-                        lhsT_scale=adj_scales[c][:, e, g, :],
-                        rhs=x2_codes[g][:].bitcast(FP8X4),
-                        rhs_scale=x2_scales[g][:],
-                        start=(g == 0),
-                        stop=(g == PASSES - 1),
-                    )
-                acc1[(c, e)] = acc
+        def diffuse(c, e):
+            acc = psum_mx.tile([P, BATCH, FEATS // RUN, RUN], F32, name="acc1", tag="mx")
+            for g in range(PASSES):
+                nc.tensor.matmul_mx(
+                    out=acc[:].rearrange("p b x i -> p (b x i)"),
+                    lhsT=adj_codes[c][:, e, g, :].bitcast(FP8X4),
+                    lhsT_scale=adj_scales[c][:, e, g, :],
+                    rhs=x2_codes[g][:].bitcast(FP8X4),
+                    rhs_scale=x2_scales[g][:],
+                    start=(g == 0),
+                    stop=(g == PASSES - 1),
+                )
+            acc1[(c, e)] = acc
 
-        def third_term(c):
-            for e in range(2):
-                nc.vector.scalar_tensor_tensor(
-                    out=rows[c][:, e, 1, :, 1, :].rearrange("p (b x) i -> p b x i", b=BATCH),
-                    in0=acc1[(c, e)][:],
-                    scalar=2.0,
-                    in1=x1_sb[c][:, :, e, :].rearrange("p b (x i) -> p b x i", i=RUN),
-                    op0=ALU.mult,
-                    op1=ALU.subtract,
+        def third_term(c, e):
+            nc.vector.scalar_tensor_tensor(
+                out=rows[c][:, e, 1, :, 1, :].rearrange("p (b x) i -> p b x i", b=BATCH),
+                in0=acc1[(c, e)][:],
+                scalar=2.0,
+                in1=x1_sb[c][:, :, e, :].rearrange("p b (x i) -> p b x i", i=RUN),
+                op0=ALU.mult,
+                op1=ALU.subtract,
+            )
+
+        def transpose_terms(c, b, e, copy=nc.scalar.copy):
+            if c not in xk_grouped:
+                xk_grouped[c] = work.tile([P, 2, HALVES, BATCH, P, 2], F32, name="xk_grouped", align_bytes=64)
+                xk_codes[c] = work.tile([P, 2, HALVES, BATCH * P], U32, name="xk_codes", align_bytes=64)
+                xk_scales[c] = work.tile([P, 2, HALVES, BATCH * P], U8, name="xk_scales", align_bytes=64)
+            xk_t = psum_tr.tile([P, HALVES, 2, P], F32, name="xk_t", tag="tr")
+            for h in range(HALVES):
+                first = (b * HALVES + h) * (P // RUN)
+                for s in range(2):
+                    words = rows[c][:, e, s, first : first + P // RUN].rearrange("p x a i -> p (x a i)")
+                    nc.tensor.transpose(xk_t[:, h, s, :], words.bitcast(F32), ident_f32[:])
+            copy(
+                out=xk_grouped[c][:, e, :, b],
+                in_=xk_t[:].rearrange("p h s n -> p h n s"),
+            )
+
+        def quantise_terms(c, e):
+            nc.vector.quantize_mx(
+                out=xk_codes[c][:, e].rearrange("p h n -> p (h n)").bitcast(FP8X4),
+                scales=xk_scales[c][:, e].rearrange("p h n -> p (h n)"),
+                in_=xk_grouped[c][:, e].rearrange("p h b n s -> p (h b n s)").bitcast(BF16),
+            )
+
+        def candidate(c, e):
+            if e == 0:
+                acc2[c] = psum_mx.tile([P, 2, BATCH * P], F32, name="acc2", tag="mx")
+                cand_t[c] = work.tile([P, 2, BATCH, P], F32, name="cand")
+            for h in range(HALVES):
+                nc.tensor.matmul_mx(
+                    out=acc2[c][:, e, :],
+                    lhsT=ck_codes[:, h, :].bitcast(FP8X4),
+                    lhsT_scale=ck_scales[:, h, :],
+                    rhs=xk_codes[c][:, e, h, :].bitcast(FP8X4),
+                    rhs_scale=xk_scales[c][:, e, h, :],
+                    start=(h == 0),
+                    stop=(h == HALVES - 1),
                 )
 
-        def transpose_terms(c):
-            grouped = work.tile([P, BATCH, HALVES, 2 * P, 2], F32, name="xk_grouped", align_bytes=64)
-            for b in range(BATCH):
-                for e in range(2):
-                    xk_t = psum_tr.tile([P, HALVES, 2, P], F32, name="xk_t", tag="tr")
-                    for h in range(HALVES):
-                        first = (b * HALVES + h) * (P // RUN)
-                        for s in range(2):
-                            words = rows[c][:, e, s, first : first + P // RUN].rearrange("p x a i -> p (x a i)")
-                            nc.tensor.transpose(xk_t[:, h, s, :], words.bitcast(F32), ident_f32[:])
-                    nc.scalar.copy(
-                        out=grouped[:, b, :, e * P : (e + 1) * P, :],
-                        in_=xk_t[:].rearrange("p h s n -> p h n s"),
-                    )
-            xk_grouped[c] = grouped
-            xk_codes[c] = work.tile([P, BATCH, HALVES, 2 * P], U32, name="xk_codes", align_bytes=64)
-            xk_scales[c] = work.tile([P, BATCH, HALVES, 2 * P], U8, name="xk_scales", align_bytes=64)
-
-        def quantise_terms(c, b):
-            nc.vector.quantize_mx(
-                out=xk_codes[c][:, b].rearrange("p h n -> p (h n)").bitcast(FP8X4),
-                scales=xk_scales[c][:, b].rearrange("p h n -> p (h n)"),
-                in_=xk_grouped[c][:, b].rearrange("p h n s -> p (h n s)").bitcast(BF16),
-            )
-
-        def candidate(c):
-            acc = psum_mx.tile([P, BATCH, 2 * P], F32, name="acc2", tag="mx")
-            for b in range(BATCH):
-                for h in range(HALVES):
-                    nc.tensor.matmul_mx(
-                        out=acc[:, b, :],
-                        lhsT=ck_codes[:, h, :].bitcast(FP8X4),
-                        lhsT_scale=ck_scales[:, h, :],
-                        rhs=xk_codes[c][:, b, h, :].bitcast(FP8X4),
-                        rhs_scale=xk_scales[c][:, b, h, :],
-                        start=(h == 0),
-                        stop=(h == HALVES - 1),
-                    )
-            cand = work.tile([P, BATCH, 2, P], F32, name="cand")
+        def squash(c, tiles):
             nc.scalar.activation(
-                out=cand[:].rearrange("p b e n -> p (b e n)"),
-                in_=acc[:].rearrange("p b n -> p (b n)"),
+                out=cand_t[c][:, tiles].rearrange("p e b n -> p (e b n)"),
+                in_=acc2[c][:, tiles, :].rearrange("p e n -> p (e n)"),
                 func=ACT.Tanh,
                 bias=bias_col[:],
                 scale=1.0,
             )
-            cand_t[c] = cand
 
         def transpose_candidate(c):
             back = psum_tr.tile([P, BATCH, 2, UNITS], F32, name="cand_n", tag="tr")
@@ -238,7 +262,7 @@ def tile_gts_gcgrucell_pc_kernel(tc, adj, x0, x1, x2, u, h_prev, c_kernel, c_bia
                 for e in range(2):
                     nc.tensor.matmul(
                         out=back[:, b, e, :],
-                        lhsT=cand_t[c][:, b, e, :],
+                        lhsT=cand_t[c][:, e, b, :],
                         rhs=ident_f32[:],
                         is_transpose=True,
                         start=False,
@@ -247,71 +271,118 @@ def tile_gts_gcgrucell_pc_kernel(tc, adj, x0, x1, x2, u, h_prev, c_kernel, c_bia
             cand_n[c] = back
 
         def blend(c):
-            minus_new = work.tile([P, BATCH * 2 * UNITS], F32, name="minus_new")
+            minus_new[c] = work.tile([P, BATCH * 2 * UNITS], F32, name="minus_new")
             nc.vector.scalar_tensor_tensor(
-                out=minus_new[:],
+                out=minus_new[c][:],
                 in0=u_sb[c][:],
                 scalar=1.0,
                 in1=cand_n[c][:].rearrange("p b e j -> p (b e j)"),
                 op0=ALU.subtract,
                 op1=ALU.mult,
             )
-            result = work.tile([P, BATCH * 2 * UNITS], F32, name="result")
-            nc.vector.tensor_tensor(out=result[:], in0=h_sb[c][:], in1=minus_new[:], op=ALU.subtract)
+
+        def store(c):
+            result = keep.tile([P, BATCH * 2 * UNITS], F32, name="result%d" % c)
+            nc.vector.tensor_tensor(out=result[:], in0=h_sb[c][:], in1=minus_new[c][:], op=ALU.subtract)
             nc.sync.dma_start(out=out_v[c], in_=result[:].rearrange("p (b x) -> p b x", b=BATCH))
 
-        transpose_adj(0)
-        regroup_x2(0)
-        place_term(0, 2)
-        place_term(1, 2)
-        quantise_adj(0)
+        V = nc.vector.tensor_copy
+        S = nc.scalar.copy
+        regroup_x2(0, 0, V)
+        place_term(0, 2, S)
+        regroup_x2(0, 1, V)
         quantise_x2(0)
-        regroup_x2(1)
+        place_term(1, 2, S)
+        regroup_x2(1, 0, S)
+        place_term(2, 2, V)
+        regroup_x2(1, 1, V)
+        for e in range(2):
+            transpose_adj(0, e)
         for h in range(HALVES):
-            ck_moved = psum_tr.tile([P, 2, 2 * UNITS], F32, name="ck_moved", tag="tr")
-            for e in range(2):
-                for a in range(2):
-                    nc.tensor.matmul(
-                        out=ck_moved[:, e, :],
-                        lhsT=move_rows[:, e, a, :],
-                        rhs=ck_sb[:, h, 2 * a : 2 * a + 2, :].rearrange("p s j -> p (s j)"),
-                        start=(a == 0),
-                        stop=(a == 1),
-                    )
-            nc.scalar.copy(out=ck_grouped[:, h], in_=ck_moved[:].rearrange("p e (s j) -> p j s e", s=2))
-        bias_t = psum_tr.tile([P, P], BF16, name="bias_t", tag="tr")
-        nc.tensor.transpose(bias_t[:], bias_rows[:], ident_bf[:])
-        transpose_adj(1)
-        place_term(2, 2)
-        place_term(3, 2)
+            move_ck(h)
+        bias_t = move_bias()
         quantise_x2(1)
-        diffuse(0)
-        nc.vector.quantize_mx(
-            out=ck_codes[:].rearrange("p h j -> p (h j)").bitcast(FP8X4),
-            scales=ck_scales[:].rearrange("p h j -> p (h j)"),
-            in_=ck_grouped[:].rearrange("p h j s e -> p (h j s e)"),
-        )
-        place_term(0, 1)
-        place_term(0, 0)
+        quantise_adj(0, slice(0, 1))
+        diffuse(0, 0)
+        place_term(0, 1, V)
+        quantise_adj(0, slice(1, 2))
+        diffuse(0, 1)
+        place_term(0, 0, S)
+        for e in range(2):
+            transpose_adj(1, e)
+        third_term(0, 0)
+        quantise_ck()
+        third_term(0, 1)
         nc.vector.tensor_copy(out=bias_col[:], in_=bias_t[:, 0:1])
-
-        for i in range(-1, PAIRS + 2):
-            if 0 <= i - 2:
-                transpose_candidate(i - 2)
-            if i + 3 < PAIRS:
-                transpose_adj(i + 3)
-            if i + 2 < PAIRS:
-                quantise_adj(i + 2)
-                diffuse(i + 2)
-            if i + 1 < PAIRS:
-                third_term(i + 1)
-                transpose_terms(i + 1)
-            if i + 2 < PAIRS:
-                place_term(i + 2, 1)
-                place_term(i + 2, 0)
-            if 0 <= i < PAIRS:
-                quantise_terms(i, 0)
-                quantise_terms(i, 1)
-                candidate(i)
-            if 0 <= i - 2:
-                blend(i - 2)
+        for e in range(2):
+            for b in range(BATCH):
+                transpose_terms(0, b, e)
+        place_term(1, 1)
+        quantise_adj(1)
+        for e in range(2):
+            transpose_adj(2, e)
+        for e in range(2):
+            diffuse(1, e)
+        place_term(1, 0)
+        place_term(2, 1)
+        quantise_terms(0, 0)
+        third_term(1, 0)
+        third_term(1, 1)
+        for e in range(2):
+            transpose_adj(3, e)
+        for e in range(2):
+            for b in range(BATCH):
+                transpose_terms(1, b, e)
+        quantise_adj(2)
+        place_term(2, 0)
+        quantise_terms(0, 1)
+        quantise_adj(3)
+        for e in range(2):
+            diffuse(2, e)
+        place_term(3, 2, S)
+        for e in range(2):
+            third_term(2, e)
+        place_term(3, 0)
+        place_term(3, 1)
+        for e in range(2):
+            diffuse(3, e)
+        for e in range(2):
+            third_term(3, e)
+        for e in range(2):
+            for b in range(BATCH):
+                transpose_terms(2, b, e)
+        for b in range(BATCH):
+            transpose_terms(3, b, 0)
+        for e in range(2):
+            candidate(0, e)
+        squash(0, slice(0, 2))
+        quantise_terms(1, 0)
+        quantise_terms(1, 1)
+        for e in range(2):
+            candidate(1, e)
+        for b in range(BATCH):
+            transpose_terms(3, b, 1)
+        squash(1, slice(0, 2))
+        quantise_terms(2, 0)
+        quantise_terms(2, 1)
+        transpose_candidate(0)
+        quantise_terms(3, 0)
+        for e in range(2):
+            candidate(2, e)
+        blend(0)
+        squash(2, slice(0, 2))
+        candidate(3, 0)
+        squash(3, slice(0, 1))
+        store(0)
+        quantise_terms(3, 1)
+        transpose_candidate(1)
+        blend(1)
+        transpose_candidate(2)
+        store(1)
+        candidate(3, 1)
+        squash(3, slice(1, 2))
+        blend(2)
+        transpose_candidate(3)
+        store(2)
+        blend(3)
+        store(3)

@@ -46,8 +46,10 @@ def tile_gts_gcgrucell_pc_kernel(tc, adj, x0, x1, x2, u, h_prev, c_kernel, c_bia
         x0_sb = [keep.tile([P, BATCH, 2, FEATS], BF16, name="x0_%d" % c) for c in range(PAIRS)]
         x1_sb = [keep.tile([P, BATCH, 2, FEATS], BF16, name="x1_%d" % c) for c in range(PAIRS)]
         x2_sb = [keep.tile([P, BATCH, 4, FEATS], BF16, name="x2_%d" % g) for g in range(PASSES)]
-        u_sb = [keep.tile([P, BATCH * 2 * UNITS], BF16, name="u%d" % c) for c in range(PAIRS)]
-        h_sb = [keep.tile([P, BATCH * 2 * UNITS], BF16, name="h%d" % c) for c in range(PAIRS)]
+        u_sb = [keep.tile([P, BATCH, 2, UNITS], BF16, name="u%d" % c) for c in range(PAIRS)]
+        h_sb = [keep.tile([P, BATCH, 2, UNITS], BF16, name="h%d" % c) for c in range(PAIRS)]
+        minus_new = [keep.tile([P, BATCH, 2, UNITS], F32, name="minus_new%d" % c) for c in range(PAIRS)]
+        result = [keep.tile([P, BATCH, 2, UNITS], F32, name="result%d" % c) for c in range(PAIRS)]
         ck_sb = keep.tile([P, HALVES, TERMS, UNITS], BF16)
         bias_rows = keep.tile([P, P], BF16)
 
@@ -68,8 +70,8 @@ def tile_gts_gcgrucell_pc_kernel(tc, adj, x0, x1, x2, u, h_prev, c_kernel, c_bia
             if c < PAIRS:
                 nc.sync.dma_start(out=x0_sb[c][:], in_=x0_v[c])
             if c >= 2:
-                nc.sync.dma_start(out=u_sb[c - 2][:].rearrange("p (b x) -> p b x", b=BATCH), in_=u_v[c - 2])
-                nc.sync.dma_start(out=h_sb[c - 2][:].rearrange("p (b x) -> p b x", b=BATCH), in_=h_v[c - 2])
+                nc.sync.dma_start(out=u_sb[c - 2][:].rearrange("p b e j -> p b (e j)"), in_=u_v[c - 2])
+                nc.sync.dma_start(out=h_sb[c - 2][:].rearrange("p b e j -> p b (e j)"), in_=h_v[c - 2])
 
         ident_f32 = keep.tile([P, P], F32)
         make_identity(nc, ident_f32[:])
@@ -108,7 +110,6 @@ def tile_gts_gcgrucell_pc_kernel(tc, adj, x0, x1, x2, u, h_prev, c_kernel, c_bia
         cand_t = {}
         acc2 = {}
         cand_n = {}
-        minus_new = {}
 
         def move_ck(h):
             ck_moved = psum_tr.tile([P, 2, 2 * UNITS], F32, name="ck_moved", tag="tr")
@@ -204,9 +205,9 @@ def tile_gts_gcgrucell_pc_kernel(tc, adj, x0, x1, x2, u, h_prev, c_kernel, c_bia
 
         def transpose_terms(c, b, e, copy=nc.scalar.copy):
             if c not in xk_grouped:
-                xk_grouped[c] = work.tile([P, 2, HALVES, BATCH, P, 2], F32, name="xk_grouped", align_bytes=64)
-                xk_codes[c] = work.tile([P, 2, HALVES, BATCH * P], U32, name="xk_codes", align_bytes=64)
-                xk_scales[c] = work.tile([P, 2, HALVES, BATCH * P], U8, name="xk_scales", align_bytes=64)
+                xk_grouped[c] = keep.tile([P, 2, HALVES, BATCH, P, 2], F32, name="xk_grouped%d" % c, align_bytes=64)
+                xk_codes[c] = keep.tile([P, 2, HALVES, BATCH * P], U32, name="xk_codes%d" % c, align_bytes=64)
+                xk_scales[c] = keep.tile([P, 2, HALVES, BATCH * P], U8, name="xk_scales%d" % c, align_bytes=64)
             xk_t = psum_tr.tile([P, HALVES, 2, P], F32, name="xk_t", tag="tr")
             for h in range(HALVES):
                 first = (b * HALVES + h) * (P // RUN)
@@ -249,42 +250,48 @@ def tile_gts_gcgrucell_pc_kernel(tc, adj, x0, x1, x2, u, h_prev, c_kernel, c_bia
                 scale=1.0,
             )
 
-        def transpose_candidate(c):
+        def transpose_candidate(c, tiles=slice(0, 2)):
             back = psum_tr.tile([P, BATCH, 2, UNITS], F32, name="cand_n", tag="tr")
             nc.tensor.matmul(
-                out=back[:].rearrange("p b e j -> p (b e j)"),
+                out=back[:, :, tiles, :],
                 lhsT=minus_ident[:],
-                rhs=h_sb[c][:],
+                rhs=h_sb[c][:, :, tiles, :],
                 start=True,
                 stop=False,
             )
             for b in range(BATCH):
-                for e in range(2):
+                for e in range(tiles.start, tiles.stop):
                     nc.tensor.matmul(
                         out=back[:, b, e, :],
                         lhsT=cand_t[c][:, e, b, :],
                         rhs=ident_f32[:],
                         is_transpose=True,
                         start=False,
-                        stop=(b == BATCH - 1 and e == 1),
+                        stop=(b == BATCH - 1 and e == tiles.stop - 1),
                     )
             cand_n[c] = back
 
-        def blend(c):
-            minus_new[c] = work.tile([P, BATCH * 2 * UNITS], F32, name="minus_new")
+        def blend(c, tiles=slice(0, 2)):
             nc.vector.scalar_tensor_tensor(
-                out=minus_new[c][:],
-                in0=u_sb[c][:],
+                out=minus_new[c][:, :, tiles, :],
+                in0=u_sb[c][:, :, tiles, :],
                 scalar=1.0,
-                in1=cand_n[c][:].rearrange("p b e j -> p (b e j)"),
+                in1=cand_n[c][:, :, tiles, :],
                 op0=ALU.subtract,
                 op1=ALU.mult,
             )
 
-        def store(c):
-            result = keep.tile([P, BATCH * 2 * UNITS], F32, name="result%d" % c)
-            nc.vector.tensor_tensor(out=result[:], in0=h_sb[c][:], in1=minus_new[c][:], op=ALU.subtract)
-            nc.sync.dma_start(out=out_v[c], in_=result[:].rearrange("p (b x) -> p b x", b=BATCH))
+        def store(c, tiles=slice(0, 2)):
+            nc.vector.tensor_tensor(
+                out=result[c][:, :, tiles, :],
+                in0=h_sb[c][:, :, tiles, :],
+                in1=minus_new[c][:, :, tiles, :],
+                op=ALU.subtract,
+            )
+            nc.sync.dma_start(
+                out=out_v[c][:, :, tiles.start * UNITS : tiles.stop * UNITS],
+                in_=result[c][:, :, tiles, :].rearrange("p b e j -> p b (e j)"),
+            )
 
         V = nc.vector.tensor_copy
         S = nc.scalar.copy
@@ -351,38 +358,40 @@ def tile_gts_gcgrucell_pc_kernel(tc, adj, x0, x1, x2, u, h_prev, c_kernel, c_bia
         for e in range(2):
             for b in range(BATCH):
                 transpose_terms(2, b, e)
-        for b in range(BATCH):
-            transpose_terms(3, b, 0)
         for e in range(2):
             candidate(0, e)
         squash(0, slice(0, 2))
-        quantise_terms(1, 0)
-        quantise_terms(1, 1)
+        for b in range(BATCH):
+            transpose_terms(3, b, 0)
+        for e in range(2):
+            quantise_terms(1, e)
+        for e in range(2):
+            quantise_terms(2, e)
+        transpose_terms(3, 0, 1, V)
+        transpose_terms(3, 1, 1)
+        transpose_candidate(0)
         for e in range(2):
             candidate(1, e)
-        for b in range(BATCH):
-            transpose_terms(3, b, 1)
         squash(1, slice(0, 2))
-        quantise_terms(2, 0)
-        quantise_terms(2, 1)
-        transpose_candidate(0)
+        blend(0)
         quantise_terms(3, 0)
+        quantise_terms(3, 1)
         for e in range(2):
             candidate(2, e)
-        blend(0)
         squash(2, slice(0, 2))
-        candidate(3, 0)
-        squash(3, slice(0, 1))
         store(0)
-        quantise_terms(3, 1)
         transpose_candidate(1)
         blend(1)
+        for e in range(2):
+            candidate(3, e)
+            squash(3, slice(e, e + 1))
         transpose_candidate(2)
-        store(1)
-        candidate(3, 1)
-        squash(3, slice(1, 2))
         blend(2)
-        transpose_candidate(3)
+        store(1)
+        transpose_candidate(3, slice(0, 1))
+        blend(3, slice(0, 1))
         store(2)
-        blend(3)
-        store(3)
+        transpose_candidate(3, slice(1, 2))
+        blend(3, slice(1, 2))
+        for e in range(2):
+            store(3, slice(e, e + 1))

@@ -55,6 +55,9 @@ def tile_gts_gcgrucell_pc_kernel(tc, adj, x0, x1, x2, u, h_prev, c_kernel, c_bia
 
         nc.vector.memset(bias_rows[:], 0.0)
         nc.scalar.dma_start(out=bias_rows[0:1, :], in_=c_bias.rearrange("(o j) -> o j", o=1))
+        warm = keep.tile([P, 1], F32)
+        nc.vector.memset(warm[:], 0.0)
+        nc.scalar.activation(out=warm[:], in_=warm[:], func=ACT.Tanh)
 
         for g in range(PASSES):
             for b in range(BATCH):
@@ -79,9 +82,6 @@ def tile_gts_gcgrucell_pc_kernel(tc, adj, x0, x1, x2, u, h_prev, c_kernel, c_bia
         make_identity(nc, ident_bf[:])
         minus_ident = keep.tile([P, P], BF16)
         nc.vector.tensor_scalar(out=minus_ident[:], in0=ident_bf[:], scalar1=-1.0, scalar2=None, op0=ALU.mult)
-        warm = keep.tile([P, 1], F32)
-        nc.vector.memset(warm[:], 0.0)
-        nc.scalar.activation(out=warm[:], in_=warm[:], func=ACT.Tanh)
         move_rows = keep.tile([P, 2, 2, P], BF16)
         nc.vector.memset(move_rows[:], 0.0)
         for e in range(2):
@@ -112,7 +112,7 @@ def tile_gts_gcgrucell_pc_kernel(tc, adj, x0, x1, x2, u, h_prev, c_kernel, c_bia
         cand_n = {}
 
         def move_ck(h):
-            ck_moved = psum_tr.tile([P, 2, 2 * UNITS], F32, name="ck_moved", tag="tr")
+            ck_moved = psum_tr.tile([P, 2, 2 * UNITS], BF16, name="ck_moved", tag="tr")
             for e in range(2):
                 for a in range(2):
                     nc.tensor.matmul(
@@ -137,7 +137,10 @@ def tile_gts_gcgrucell_pc_kernel(tc, adj, x0, x1, x2, u, h_prev, c_kernel, c_bia
             return bias_t
 
         def regroup_x2(g, b, copy):
-            copy(out=x2_grouped[g][:, b], in_=x2_sb[g][:, b].rearrange("p t f -> p f t"))
+            copy(
+                out=x2_grouped[g][:, b].rearrange("p (q i) t -> p q t i", i=4),
+                in_=x2_sb[g][:, b].rearrange("p t (q i) -> p q t i", i=4),
+            )
 
         def quantise_x2(g):
             nc.vector.quantize_mx(
@@ -303,12 +306,13 @@ def tile_gts_gcgrucell_pc_kernel(tc, adj, x0, x1, x2, u, h_prev, c_kernel, c_bia
         regroup_x2(1, 0, S)
         place_term(2, 2, V)
         regroup_x2(1, 1, V)
+        bias_t = move_bias()
         for e in range(2):
             transpose_adj(0, e)
         for h in range(HALVES):
             move_ck(h)
-        bias_t = move_bias()
         quantise_x2(1)
+        nc.vector.tensor_copy(out=bias_col[:], in_=bias_t[:, 0:1])
         quantise_adj(0, slice(0, 1))
         diffuse(0, 0)
         place_term(0, 1, V)
@@ -320,7 +324,6 @@ def tile_gts_gcgrucell_pc_kernel(tc, adj, x0, x1, x2, u, h_prev, c_kernel, c_bia
         third_term(0, 0)
         quantise_ck()
         third_term(0, 1)
-        nc.vector.tensor_copy(out=bias_col[:], in_=bias_t[:, 0:1])
         for e in range(2):
             for b in range(BATCH):
                 transpose_terms(0, b, e)

@@ -298,97 +298,97 @@ def tile_gts_gcgrucell_pc_kernel(tc, adj, x0, x1, x2, u, h_prev, c_kernel, c_bia
 
         V = nc.vector.tensor_copy
         S = nc.scalar.copy
+        bias_t = move_bias()
         regroup_x2(0, 0, V)
-        place_term(0, 2, S)
-        regroup_x2(0, 1, V)
+        regroup_x2(0, 1, S)
+        place_term(0, 2, V)
+        regroup_x2(1, 0, V)
+        regroup_x2(1, 1, V)
         quantise_x2(0)
         place_term(1, 2, S)
-        regroup_x2(1, 0, S)
-        place_term(2, 2, V)
-        regroup_x2(1, 1, V)
-        bias_t = move_bias()
-        for e in range(2):
-            transpose_adj(0, e)
-        for h in range(HALVES):
-            move_ck(h)
         quantise_x2(1)
         nc.vector.tensor_copy(out=bias_col[:], in_=bias_t[:, 0:1])
-        quantise_adj(0, slice(0, 1))
-        diffuse(0, 0)
+        for e in range(2):
+            transpose_adj(0, e)
+        move_ck(0)
+        for e in range(2):
+            place_term(2 + e, 2, V)
+        for e in range(2):
+            quantise_adj(0, slice(e, e + 1))
+            diffuse(0, e)
         place_term(0, 1, V)
-        quantise_adj(0, slice(1, 2))
-        diffuse(0, 1)
-        place_term(0, 0, S)
         for e in range(2):
             transpose_adj(1, e)
-        third_term(0, 0)
-        quantise_ck()
-        third_term(0, 1)
+        move_ck(1)
+        for e in range(2):
+            third_term(0, e)
+        place_term(0, 0, V)
         for e in range(2):
             for b in range(BATCH):
                 transpose_terms(0, b, e)
-        place_term(1, 1)
         quantise_adj(1)
+        quantise_ck()
+        place_term(1, 1, V)
         for e in range(2):
             transpose_adj(2, e)
         for e in range(2):
             diffuse(1, e)
-        place_term(1, 0)
-        place_term(2, 1)
+        place_term(1, 0, V)
+        for e in range(2):
+            third_term(1, e)
+        for b in range(BATCH):
+            transpose_terms(1, b, 0)
         quantise_terms(0, 0)
-        third_term(1, 0)
-        third_term(1, 1)
+        quantise_terms(0, 1)
         for e in range(2):
             transpose_adj(3, e)
-        for e in range(2):
-            for b in range(BATCH):
-                transpose_terms(1, b, e)
+        for b in range(BATCH):
+            transpose_terms(1, b, 1)
         quantise_adj(2)
-        place_term(2, 0)
-        quantise_terms(0, 1)
-        quantise_adj(3)
-        for e in range(2):
-            diffuse(2, e)
-        place_term(3, 2, S)
-        for e in range(2):
-            third_term(2, e)
-        place_term(3, 0)
-        place_term(3, 1)
-        for e in range(2):
-            diffuse(3, e)
-        for e in range(2):
-            third_term(3, e)
-        for e in range(2):
-            for b in range(BATCH):
-                transpose_terms(2, b, e)
         for e in range(2):
             candidate(0, e)
         squash(0, slice(0, 2))
-        for b in range(BATCH):
-            transpose_terms(3, b, 0)
+        place_term(2, 1, V)
         for e in range(2):
-            quantise_terms(1, e)
+            diffuse(2, e)
+        quantise_adj(3)
+        place_term(2, 0, V)
         for e in range(2):
-            quantise_terms(2, e)
-        transpose_terms(3, 0, 1, V)
-        transpose_terms(3, 1, 1)
-        transpose_candidate(0)
+            diffuse(3, e)
+        third_term(2, 0)
+        quantise_terms(1, 0)
+        third_term(2, 1)
+        place_term(3, 1, S)
+        place_term(3, 0, S)
+        for e in range(2):
+            for b in range(BATCH):
+                transpose_terms(2, b, e)
+        third_term(3, 0)
+        quantise_terms(1, 1)
+        third_term(3, 1)
+        transpose_terms(3, 0, 0, V)
         for e in range(2):
             candidate(1, e)
         squash(1, slice(0, 2))
+        transpose_terms(3, 1, 0, S)
+        transpose_candidate(0)
+        for b in range(BATCH):
+            transpose_terms(3, b, 1)
+        for e in range(2):
+            quantise_terms(2, e)
+            candidate(2, e)
         blend(0)
         quantise_terms(3, 0)
-        quantise_terms(3, 1)
-        for e in range(2):
-            candidate(2, e)
-        squash(2, slice(0, 2))
         store(0)
+        squash(2, slice(0, 2))
         transpose_candidate(1)
+        quantise_terms(3, 1)
+        candidate(3, 0)
+        squash(3, slice(0, 1))
         blend(1)
-        for e in range(2):
-            candidate(3, e)
-            squash(3, slice(e, e + 1))
         transpose_candidate(2)
+        candidate(3, 1)
+        squash(3, slice(1, 2))
         blend(2)
         store(1)
         transpose_candidate(3, slice(0, 1))

@@ -330,9 +330,9 @@ def tile_gts_gcgrucell_pc_kernel(tc, adj, x0, x1, x2, u, h_prev, c_kernel, c_bia
         quantise_ck()
         place_term(1, 1, V)
         for e in range(2):
-            transpose_adj(2, e)
-        for e in range(2):
             diffuse(1, e)
+        for e in range(2):
+            transpose_adj(2, e)
         place_term(1, 0, V)
         for e in range(2):
             third_term(1, e)
@@ -342,17 +342,17 @@ def tile_gts_gcgrucell_pc_kernel(tc, adj, x0, x1, x2, u, h_prev, c_kernel, c_bia
         quantise_terms(0, 1)
         for e in range(2):
             transpose_adj(3, e)
-        for b in range(BATCH):
-            transpose_terms(1, b, 1)
         quantise_adj(2)
         for e in range(2):
             candidate(0, e)
         squash(0, slice(0, 2))
+        for b in range(BATCH):
+            transpose_terms(1, b, 1)
         place_term(2, 1, V)
         for e in range(2):
             diffuse(2, e)
-        quantise_adj(3)
         place_term(2, 0, V)
+        quantise_adj(3)
         for e in range(2):
             diffuse(3, e)
         third_term(2, 0)

@@ -50,7 +50,7 @@ def tile_gts_gcgrucell_pc_kernel(tc, adj, x0, x1, x2, u, h_prev, c_kernel, c_bia
         h_sb = [keep.tile([P, BATCH, 2, UNITS], BF16, name="h%d" % c) for c in range(PAIRS)]
         minus_new = [keep.tile([P, BATCH, 2, UNITS], F32, name="minus_new%d" % c) for c in range(PAIRS)]
         result = [keep.tile([P, BATCH, 2, UNITS], F32, name="result%d" % c) for c in range(PAIRS)]
-        ck_sb = keep.tile([P, HALVES, TERMS, UNITS], BF16)
+        ck_sb = keep.tile([P, HALVES, 2, 2 * UNITS], BF16)
         bias_rows = keep.tile([P, P], BF16)
 
         nc.vector.memset(bias_rows[:], 0.0)
@@ -64,17 +64,24 @@ def tile_gts_gcgrucell_pc_kernel(tc, adj, x0, x1, x2, u, h_prev, c_kernel, c_bia
                 nc.sync.dma_start(out=x2_sb[g][:, b].rearrange("p (w e) f -> p w (e f)", e=2), in_=x2_v[g, b])
         for e in range(2):
             nc.sync.dma_start(out=adj_sb[0][:, e, :], in_=adj_v[0][:, e * NODES : (e + 1) * NODES])
-        nc.sync.dma_start(out=ck_sb[:], in_=c_kernel.rearrange("(h p k) j -> p h (k j)", h=HALVES, p=P, k=TERMS))
-        for c in range(PAIRS + 2):
-            if c < PAIRS:
-                nc.sync.dma_start(out=x1_sb[c][:], in_=x1_v[c])
-            if c + 1 < PAIRS:
-                nc.sync.dma_start(out=adj_sb[c + 1][:], in_=adj_v[c + 1])
-            if c < PAIRS:
-                nc.sync.dma_start(out=x0_sb[c][:], in_=x0_v[c])
-            if c >= 2:
-                nc.sync.dma_start(out=u_sb[c - 2][:].rearrange("p b e j -> p b (e j)"), in_=u_v[c - 2])
-                nc.sync.dma_start(out=h_sb[c - 2][:].rearrange("p b e j -> p b (e j)"), in_=h_v[c - 2])
+        ck_v = c_kernel.rearrange("(h q e a s) j -> h a q e (s j)", h=HALVES, q=P // 2, e=2, a=2, s=2)
+        for h in range(HALVES):
+            for a in range(2):
+                nc.sync.dma_start(out=ck_sb[a:P:2, h], in_=ck_v[h, a])
+        nc.sync.dma_start(out=x1_sb[0][:], in_=x1_v[0])
+        nc.sync.dma_start(out=adj_sb[1][:], in_=adj_v[1])
+        nc.sync.dma_start(out=x0_sb[0][:], in_=x0_v[0])
+        nc.sync.dma_start(out=x1_sb[1][:], in_=x1_v[1])
+        nc.sync.dma_start(out=adj_sb[2][:], in_=adj_v[2])
+        nc.sync.dma_start(out=x0_sb[1][:], in_=x0_v[1])
+        nc.sync.dma_start(out=adj_sb[3][:], in_=adj_v[3])
+        nc.sync.dma_start(out=x1_sb[2][:], in_=x1_v[2])
+        nc.sync.dma_start(out=x0_sb[2][:], in_=x0_v[2])
+        nc.sync.dma_start(out=x1_sb[3][:], in_=x1_v[3])
+        nc.sync.dma_start(out=x0_sb[3][:], in_=x0_v[3])
+        for c in range(PAIRS):
+            nc.sync.dma_start(out=u_sb[c][:].rearrange("p b e j -> p b (e j)"), in_=u_v[c])
+            nc.sync.dma_start(out=h_sb[c][:].rearrange("p b e j -> p b (e j)"), in_=h_v[c])
 
         ident_f32 = keep.tile([P, P], F32)
         make_identity(nc, ident_f32[:])
@@ -82,14 +89,11 @@ def tile_gts_gcgrucell_pc_kernel(tc, adj, x0, x1, x2, u, h_prev, c_kernel, c_bia
         make_identity(nc, ident_bf[:])
         minus_ident = keep.tile([P, P], BF16)
         nc.vector.tensor_scalar(out=minus_ident[:], in0=ident_bf[:], scalar1=-1.0, scalar2=None, op0=ALU.mult)
-        move_rows = keep.tile([P, 2, 2, P], BF16)
-        nc.vector.memset(move_rows[:], 0.0)
-        for e in range(2):
-            for a in range(2):
-                nc.vector.tensor_copy(
-                    out=move_rows[:, e, a, :].rearrange("p (B x w) -> p B x w", x=2, w=RUN // 2)[:, :, a, :],
-                    in_=ident_bf[:].rearrange("p (B w y) -> p B w y", w=RUN // 2, y=2)[:, :, :, e],
-                )
+        move_rows = keep.tile([P, P], BF16)
+        nc.vector.tensor_copy(
+            out=move_rows[:].rearrange("p (B a w) -> p B a w", a=2, w=RUN // 2),
+            in_=ident_bf[:].rearrange("p (B w a) -> p B a w", w=RUN // 2, a=2),
+        )
 
         x2_grouped = [keep.tile([P, BATCH, FEATS, 4], BF16, name="x2_grouped%d" % g, align_bytes=64) for g in range(PASSES)]
         x2_codes = [keep.tile([P, BATCH * FEATS], U32, name="x2_codes%d" % g, align_bytes=64) for g in range(PASSES)]
@@ -111,18 +115,14 @@ def tile_gts_gcgrucell_pc_kernel(tc, adj, x0, x1, x2, u, h_prev, c_kernel, c_bia
         acc2 = {}
         cand_n = {}
 
-        def move_ck(h):
-            ck_moved = psum_tr.tile([P, 2, 2 * UNITS], BF16, name="ck_moved", tag="tr")
-            for e in range(2):
-                for a in range(2):
+        def move_ck():
+            ck_moved = psum_tr.tile([P, HALVES, 2, 2 * UNITS], BF16, name="ck_moved", tag="tr")
+            for h in range(HALVES):
+                for e in range(2):
                     nc.tensor.matmul(
-                        out=ck_moved[:, e, :],
-                        lhsT=move_rows[:, e, a, :],
-                        rhs=ck_sb[:, h, 2 * a : 2 * a + 2, :].rearrange("p s j -> p (s j)"),
-                        start=(a == 0),
-                        stop=(a == 1),
+                        out=ck_moved[:, h, e, :], lhsT=move_rows[:], rhs=ck_sb[:, h, e, :], start=True, stop=True
                     )
-            nc.scalar.copy(out=ck_grouped[:, h], in_=ck_moved[:].rearrange("p e (s j) -> p j s e", s=2))
+            nc.scalar.copy(out=ck_grouped[:], in_=ck_moved[:].rearrange("p h e (s j) -> p h j s e", s=2))
 
         def quantise_ck():
             nc.vector.quantize_mx(
@@ -310,7 +310,7 @@ def tile_gts_gcgrucell_pc_kernel(tc, adj, x0, x1, x2, u, h_prev, c_kernel, c_bia
         nc.vector.tensor_copy(out=bias_col[:], in_=bias_t[:, 0:1])
         for e in range(2):
             transpose_adj(0, e)
-        move_ck(0)
+        move_ck()
         for e in range(2):
             place_term(2 + e, 2, V)
         for e in range(2):
@@ -319,14 +319,14 @@ def tile_gts_gcgrucell_pc_kernel(tc, adj, x0, x1, x2, u, h_prev, c_kernel, c_bia
         place_term(0, 1, V)
         for e in range(2):
             transpose_adj(1, e)
-        move_ck(1)
-        for e in range(2):
-            third_term(0, e)
+        third_term(0, 0)
         place_term(0, 0, V)
+        third_term(0, 1)
         for e in range(2):
             for b in range(BATCH):
                 transpose_terms(0, b, e)
-        quantise_adj(1)
+        for e in range(2):
+            quantise_adj(1, slice(e, e + 1))
         quantise_ck()
         place_term(1, 1, V)
         for e in range(2):
@@ -352,7 +352,8 @@ def tile_gts_gcgrucell_pc_kernel(tc, adj, x0, x1, x2, u, h_prev, c_kernel, c_bia
         for e in range(2):
             diffuse(2, e)
         place_term(2, 0, V)
-        quantise_adj(3)
+        for e in range(2):
+            quantise_adj(3, slice(e, e + 1))
         for e in range(2):
             diffuse(3, e)
         third_term(2, 0)
@@ -367,10 +368,10 @@ def tile_gts_gcgrucell_pc_kernel(tc, adj, x0, x1, x2, u, h_prev, c_kernel, c_bia
         quantise_terms(1, 1)
         third_term(3, 1)
         transpose_terms(3, 0, 0, V)
+        transpose_terms(3, 1, 0, S)
         for e in range(2):
             candidate(1, e)
         squash(1, slice(0, 2))
-        transpose_terms(3, 1, 0, S)
         transpose_candidate(0)
         for b in range(BATCH):
             transpose_terms(3, b, 1)

from contextlib import ExitStack

import concourse.mybir as mybir
from concourse.masks import make_identity

F32 = mybir.dt.float32
BF16 = mybir.dt.bfloat16
U32 = mybir.dt.uint32
U8 = mybir.dt.uint8
FP8X4 = mybir.dt.float8_e4m3fn_x4
ALU = mybir.AluOpType
ACT = mybir.ActivationFunctionType

P = 128
BATCH = 2
NODES = 1024
FEATS = 256
UNITS = 128
TERMS = 4
HALVES = FEATS // P
PASSES = NODES // (4 * P)
PAIRS = NODES // (2 * P)
RUN = 8
RUNS = BATCH * FEATS // RUN
FLOPS = 2 * NODES * NODES * BATCH * FEATS + 2 * BATCH * NODES * TERMS * FEATS * UNITS


def tile_gts_gcgrucell_pc_kernel(tc, adj, x0, x1, x2, u, h_prev, c_kernel, c_bias, out):
    nc = tc.nc
    adj_v = adj.rearrange("(c p e) m -> c p (e m)", c=PAIRS, p=P, e=2)
    x0_v = x0.rearrange("b (c p e) f -> c p b (e f)", c=PAIRS, p=P, e=2)
    x1_v = x1.rearrange("b (c p e) f -> c p b (e f)", c=PAIRS, p=P, e=2)
    x2_v = x2.rearrange("b (g w p e) f -> g b p w (e f)", g=PASSES, w=2, p=P, e=2)
    u_v = u.rearrange("b (c p e j) -> c p b (e j)", c=PAIRS, p=P, e=2, j=UNITS)
    h_v = h_prev.rearrange("b (c p e j) -> c p b (e j)", c=PAIRS, p=P, e=2, j=UNITS)
    out_v = out.rearrange("b (c p e j) -> c p b (e j)", c=PAIRS, p=P, e=2, j=UNITS)

    with ExitStack() as ctx:
        keep = ctx.enter_context(tc.tile_pool(name="keep", bufs=1))
        work = ctx.enter_context(tc.tile_pool(name="work", bufs=2))
        psum_tr = ctx.enter_context(tc.psum_pool(name="psum_tr", bufs=5))
        psum_mx = ctx.enter_context(tc.psum_pool(name="psum_mx", bufs=3))
        ctx.enter_context(tc.manual_schedule())

        adj_sb = [keep.tile([P, 2, NODES], BF16, name="adj%d" % c) for c in range(PAIRS)]
        x0_sb = [keep.tile([P, BATCH, 2, FEATS], BF16, name="x0_%d" % c) for c in range(PAIRS)]
        x1_sb = [keep.tile([P, BATCH, 2, FEATS], BF16, name="x1_%d" % c) for c in range(PAIRS)]
        x2_sb = [keep.tile([P, BATCH, 4, FEATS], BF16, name="x2_%d" % g) for g in range(PASSES)]
        u_sb = [keep.tile([P, BATCH, 2, UNITS], BF16, name="u%d" % c) for c in range(PAIRS)]
        h_sb = [keep.tile([P, BATCH, 2, UNITS], BF16, name="h%d" % c) for c in range(PAIRS)]
        minus_new = [keep.tile([P, BATCH, 2, UNITS], F32, name="minus_new%d" % c) for c in range(PAIRS)]
        result = [keep.tile([P, BATCH, 2, UNITS], F32, name="result%d" % c) for c in range(PAIRS)]
        ck_sb = keep.tile([P, HALVES, 2, 2 * UNITS], BF16)
        bias_rows = keep.tile([P, P], BF16)

        nc.vector.memset(bias_rows[:], 0.0)
        nc.scalar.dma_start(out=bias_rows[0:1, :], in_=c_bias.rearrange("(o j) -> o j", o=1))
        warm = keep.tile([P, 1], F32)
        nc.vector.memset(warm[:], 0.0)
        nc.scalar.activation(out=warm[:], in_=warm[:], func=ACT.Tanh)

        for g in range(PASSES):
            for b in range(BATCH):
                nc.sync.dma_start(out=x2_sb[g][:, b].rearrange("p (w e) f -> p w (e f)", e=2), in_=x2_v[g, b])
        for e in range(2):
            nc.sync.dma_start(out=adj_sb[0][:, e, :], in_=adj_v[0][:, e * NODES : (e + 1) * NODES])
        ck_v = c_kernel.rearrange("(h q e a s) j -> h a q e (s j)", h=HALVES, q=P // 2, e=2, a=2, s=2)
        for h in range(HALVES):
            for a in range(2):
                nc.sync.dma_start(out=ck_sb[a:P:2, h], in_=ck_v[h, a])
        nc.sync.dma_start(out=x1_sb[0][:], in_=x1_v[0])
        nc.sync.dma_start(out=adj_sb[1][:], in_=adj_v[1])
        nc.sync.dma_start(out=x0_sb[0][:], in_=x0_v[0])
        nc.sync.dma_start(out=x1_sb[1][:], in_=x1_v[1])
        nc.sync.dma_start(out=adj_sb[2][:], in_=adj_v[2])
        nc.sync.dma_start(out=x0_sb[1][:], in_=x0_v[1])
        nc.sync.dma_start(out=adj_sb[3][:], in_=adj_v[3])
        nc.sync.dma_start(out=x1_sb[2][:], in_=x1_v[2])
        nc.sync.dma_start(out=x0_sb[2][:], in_=x0_v[2])
        nc.sync.dma_start(out=x1_sb[3][:], in_=x1_v[3])
        nc.sync.dma_start(out=x0_sb[3][:], in_=x0_v[3])
        for c in range(PAIRS):
            nc.sync.dma_start(out=u_sb[c][:].rearrange("p b e j -> p b (e j)"), in_=u_v[c])
            nc.sync.dma_start(out=h_sb[c][:].rearrange("p b e j -> p b (e j)"), in_=h_v[c])

        ident_f32 = keep.tile([P, P], F32)
        make_identity(nc, ident_f32[:])
        ident_bf = keep.tile([P, P], BF16)
        make_identity(nc, ident_bf[:])
        minus_ident = keep.tile([P, P], BF16)
        nc.vector.tensor_scalar(out=minus_ident[:], in0=ident_bf[:], scalar1=-1.0, scalar2=None, op0=ALU.mult)
        move_rows = keep.tile([P, P], BF16)
        nc.vector.tensor_copy(
            out=move_rows[:].rearrange("p (B a w) -> p B a w", a=2, w=RUN // 2),
            in_=ident_bf[:].rearrange("p (B w a) -> p B a w", w=RUN // 2, a=2),
        )

        x2_grouped = [keep.tile([P, BATCH, FEATS, 4], BF16, name="x2_grouped%d" % g, align_bytes=64) for g in range(PASSES)]
        x2_codes = [keep.tile([P, BATCH * FEATS], U32, name="x2_codes%d" % g, align_bytes=64) for g in range(PASSES)]
        x2_scales = [keep.tile([P, BATCH * FEATS], U8, name="x2_scales%d" % g, align_bytes=64) for g in range(PASSES)]
        rows = [keep.tile([P, 2, 2, RUNS, 2, RUN], BF16, name="rows%d" % c) for c in range(PAIRS)]
        ck_grouped = keep.tile([P, HALVES, UNITS, 2, 2], BF16, align_bytes=64)
        ck_codes = keep.tile([P, HALVES, UNITS], U32, align_bytes=64)
        ck_scales = keep.tile([P, HALVES, UNITS], U8, align_bytes=64)
        bias_col = keep.tile([P, 1], F32)

        adj_grouped = {}
        adj_codes = {}
        adj_scales = {}
        acc1 = {}
        xk_grouped = {}
        xk_codes = {}
        xk_scales = {}
        cand_t = {}
        acc2 = {}
        cand_n = {}

        def move_ck():
            ck_moved = psum_tr.tile([P, HALVES, 2, 2 * UNITS], BF16, name="ck_moved", tag="tr")
            for h in range(HALVES):
                for e in range(2):
                    nc.tensor.matmul(
                        out=ck_moved[:, h, e, :], lhsT=move_rows[:], rhs=ck_sb[:, h, e, :], start=True, stop=True
                    )
            nc.scalar.copy(out=ck_grouped[:], in_=ck_moved[:].rearrange("p h e (s j) -> p h j s e", s=2))

        def quantise_ck():
            nc.vector.quantize_mx(
                out=ck_codes[:].rearrange("p h j -> p (h j)").bitcast(FP8X4),
                scales=ck_scales[:].rearrange("p h j -> p (h j)"),
                in_=ck_grouped[:].rearrange("p h j s e -> p (h j s e)"),
            )

        def move_bias():
            bias_t = psum_tr.tile([P, P], BF16, name="bias_t", tag="tr")
            nc.tensor.transpose(bias_t[:], bias_rows[:], ident_bf[:])
            return bias_t

        def regroup_x2(g, b, copy):
            copy(
                out=x2_grouped[g][:, b].rearrange("p (q i) t -> p q t i", i=4),
                in_=x2_sb[g][:, b].rearrange("p t (q i) -> p q t i", i=4),
            )

        def quantise_x2(g):
            nc.vector.quantize_mx(
                out=x2_codes[g][:].bitcast(FP8X4),
                scales=x2_scales[g][:],
                in_=x2_grouped[g][:].rearrange("p b f t -> p (b f t)"),
            )

        def place_term(c, k, copy=nc.vector.tensor_copy):
            if k == 2:
                term = x2_sb[c // 2][:, :, 2 * (c % 2) : 2 * (c % 2) + 2, :]
            elif k == 1:
                term = x1_sb[c][:]
            else:
                term = x0_sb[c][:]
            copy(
                out=rows[c][:, :, k % 2, :, k // 2, :].rearrange("p e (b x) i -> p e b x i", b=BATCH),
                in_=term.rearrange("p b e (x i) -> p e b x i", i=RUN),
            )

        def transpose_adj(c, e):
            if e == 0:
                adj_grouped[c] = work.tile([P, 2, PASSES, P, 2], F32, name="adj_grouped", align_bytes=64)
            words = adj_sb[c][:, e, :].bitcast(F32)
            adj_t = psum_tr.tile([P, PASSES, 2, P], F32, name="adj_t", tag="tr")
            for g in range(PASSES):
                for w in range(2):
                    first = (2 * g + w) * P
                    nc.tensor.transpose(adj_t[:, g, w, :], words[:, first : first + P], ident_f32[:])
            nc.scalar.copy(out=adj_grouped[c][:, e], in_=adj_t[:].rearrange("p g w n -> p g n w"))

        def quantise_adj(c, tiles=slice(0, 2)):
            if c not in adj_codes:
                adj_codes[c] = work.tile([P, 2, PASSES, P], U32, name="adj_codes", align_bytes=64)
                adj_scales[c] = work.tile([P, 2, PASSES, P], U8, name="adj_scales", align_bytes=64)
            nc.vector.quantize_mx(
                out=adj_codes[c][:, tiles].rearrange("p e g n -> p (e g n)").bitcast(FP8X4),
                scales=adj_scales[c][:, tiles].rearrange("p e g n -> p (e g n)"),
                in_=adj_grouped[c][:, tiles].rearrange("p e g n w -> p (e g n w)").bitcast(BF16),
            )

        def diffuse(c, e):
            acc = psum_mx.tile([P, BATCH, FEATS // RUN, RUN], F32, name="acc1", tag="mx")
            for g in range(PASSES):
                nc.tensor.matmul_mx(
                    out=acc[:].rearrange("p b x i -> p (b x i)"),
                    lhsT=adj_codes[c][:, e, g, :].bitcast(FP8X4),
                    lhsT_scale=adj_scales[c][:, e, g, :],
                    rhs=x2_codes[g][:].bitcast(FP8X4),
                    rhs_scale=x2_scales[g][:],
                    start=(g == 0),
                    stop=(g == PASSES - 1),
                )
            acc1[(c, e)] = acc

        def third_term(c, e):
            nc.vector.scalar_tensor_tensor(
                out=rows[c][:, e, 1, :, 1, :].rearrange("p (b x) i -> p b x i", b=BATCH),
                in0=acc1[(c, e)][:],
                scalar=2.0,
                in1=x1_sb[c][:, :, e, :].rearrange("p b (x i) -> p b x i", i=RUN),
                op0=ALU.mult,
                op1=ALU.subtract,
            )

        def transpose_terms(c, b, e, copy=nc.scalar.copy):
            if c not in xk_grouped:
                xk_grouped[c] = keep.tile([P, 2, HALVES, BATCH, P, 2], F32, name="xk_grouped%d" % c, align_bytes=64)
                xk_codes[c] = keep.tile([P, 2, HALVES, BATCH * P], U32, name="xk_codes%d" % c, align_bytes=64)
                xk_scales[c] = keep.tile([P, 2, HALVES, BATCH * P], U8, name="xk_scales%d" % c, align_bytes=64)
            xk_t = psum_tr.tile([P, HALVES, 2, P], F32, name="xk_t", tag="tr")
            for h in range(HALVES):
                first = (b * HALVES + h) * (P // RUN)
                for s in range(2):
                    words = rows[c][:, e, s, first : first + P // RUN].rearrange("p x a i -> p (x a i)")
                    nc.tensor.transpose(xk_t[:, h, s, :], words.bitcast(F32), ident_f32[:])
            copy(
                out=xk_grouped[c][:, e, :, b],
                in_=xk_t[:].rearrange("p h s n -> p h n s"),
            )

        def quantise_terms(c, e):
            nc.vector.quantize_mx(
                out=xk_codes[c][:, e].rearrange("p h n -> p (h n)").bitcast(FP8X4),
                scales=xk_scales[c][:, e].rearrange("p h n -> p (h n)"),
                in_=xk_grouped[c][:, e].rearrange("p h b n s -> p (h b n s)").bitcast(BF16),
            )

        def candidate(c, e):
            if e == 0:
                acc2[c] = psum_mx.tile([P, 2, BATCH * P], F32, name="acc2", tag="mx")
                cand_t[c] = work.tile([P, 2, BATCH, P], F32, name="cand")
            for h in range(HALVES):
                nc.tensor.matmul_mx(
                    out=acc2[c][:, e, :],
                    lhsT=ck_codes[:, h, :].bitcast(FP8X4),
                    lhsT_scale=ck_scales[:, h, :],
                    rhs=xk_codes[c][:, e, h, :].bitcast(FP8X4),
                    rhs_scale=xk_scales[c][:, e, h, :],
                    start=(h == 0),
                    stop=(h == HALVES - 1),
                )

        def squash(c, tiles):
            nc.scalar.activation(
                out=cand_t[c][:, tiles].rearrange("p e b n -> p (e b n)"),
                in_=acc2[c][:, tiles, :].rearrange("p e n -> p (e n)"),
                func=ACT.Tanh,
                bias=bias_col[:],
                scale=1.0,
            )

        def transpose_candidate(c, tiles=slice(0, 2)):
            back = psum_tr.tile([P, BATCH, 2, UNITS], F32, name="cand_n", tag="tr")
            nc.tensor.matmul(
                out=back[:, :, tiles, :],
                lhsT=minus_ident[:],
                rhs=h_sb[c][:, :, tiles, :],
                start=True,
                stop=False,
            )
            for b in range(BATCH):
                for e in range(tiles.start, tiles.stop):
                    nc.tensor.matmul(
                        out=back[:, b, e, :],
                        lhsT=cand_t[c][:, e, b, :],
                        rhs=ident_f32[:],
                        is_transpose=True,
                        start=False,
                        stop=(b == BATCH - 1 and e == tiles.stop - 1),
                    )
            cand_n[c] = back

        def blend(c, tiles=slice(0, 2)):
            nc.vector.scalar_tensor_tensor(
                out=minus_new[c][:, :, tiles, :],
                in0=u_sb[c][:, :, tiles, :],
                scalar=1.0,
                in1=cand_n[c][:, :, tiles, :],
                op0=ALU.subtract,
                op1=ALU.mult,
            )

        def store(c, tiles=slice(0, 2)):
            nc.vector.tensor_tensor(
                out=result[c][:, :, tiles, :],
                in0=h_sb[c][:, :, tiles, :],
                in1=minus_new[c][:, :, tiles, :],
                op=ALU.subtract,
            )
            nc.sync.dma_start(
                out=out_v[c][:, :, tiles.start * UNITS : tiles.stop * UNITS],
                in_=result[c][:, :, tiles, :].rearrange("p b e j -> p b (e j)"),
            )

        V = nc.vector.tensor_copy
        S = nc.scalar.copy
        bias_t = move_bias()
        regroup_x2(0, 0, V)
        regroup_x2(0, 1, S)
        place_term(0, 2, V)
        regroup_x2(1, 0, V)
        regroup_x2(1, 1, V)
        quantise_x2(0)
        place_term(1, 2, S)
        quantise_x2(1)
        nc.vector.tensor_copy(out=bias_col[:], in_=bias_t[:, 0:1])
        for e in range(2):
            transpose_adj(0, e)
        move_ck()
        for e in range(2):
            place_term(2 + e, 2, V)
        for e in range(2):
            quantise_adj(0, slice(e, e + 1))
            diffuse(0, e)
        place_term(0, 1, V)
        for e in range(2):
            transpose_adj(1, e)
        third_term(0, 0)
        place_term(0, 0, V)
        third_term(0, 1)
        for e in range(2):
            for b in range(BATCH):
                transpose_terms(0, b, e)
        for e in range(2):
            quantise_adj(1, slice(e, e + 1))
        quantise_ck()
        place_term(1, 1, V)
        for e in range(2):
            diffuse(1, e)
        for e in range(2):
            transpose_adj(2, e)
        place_term(1, 0, V)
        for e in range(2):
            third_term(1, e)
        for b in range(BATCH):
            transpose_terms(1, b, 0)
        quantise_terms(0, 0)
        quantise_terms(0, 1)
        for e in range(2):
            transpose_adj(3, e)
        quantise_adj(2)
        for e in range(2):
            candidate(0, e)
        squash(0, slice(0, 2))
        for b in range(BATCH):
            transpose_terms(1, b, 1)
        place_term(2, 1, V)
        for e in range(2):
            diffuse(2, e)
        place_term(2, 0, V)
        for e in range(2):
            quantise_adj(3, slice(e, e + 1))
        for e in range(2):
            diffuse(3, e)
        third_term(2, 0)
        quantise_terms(1, 0)
        third_term(2, 1)
        place_term(3, 1, S)
        place_term(3, 0, S)
        for e in range(2):
            for b in range(BATCH):
                transpose_terms(2, b, e)
        third_term(3, 0)
        quantise_terms(1, 1)
        third_term(3, 1)
        transpose_terms(3, 0, 0, V)
        transpose_terms(3, 1, 0, S)
        for e in range(2):
            candidate(1, e)
        squash(1, slice(0, 2))
        transpose_candidate(0)
        for b in range(BATCH):
            transpose_terms(3, b, 1)
        for e in range(2):
            quantise_terms(2, e)
            candidate(2, e)
        blend(0)
        quantise_terms(3, 0)
        store(0)
        squash(2, slice(0, 2))
        transpose_candidate(1)
        quantise_terms(3, 1)
        candidate(3, 0)
        squash(3, slice(0, 1))
        blend(1)
        transpose_candidate(2)
        candidate(3, 1)
        squash(3, slice(1, 2))
        blend(2)
        store(1)
        transpose_candidate(3, slice(0, 1))
        blend(3, slice(0, 1))
        store(2)
        transpose_candidate(3, slice(1, 2))
        blend(3, slice(1, 2))
        for e in range(2):
            store(3, slice(e, e + 1))
